import numpy as np
import ml_dtypes


def mxq(x, axis, fmt="e4m3"):
    dtype, down = {"e4m3": (ml_dtypes.float8_e4m3fn, 7), "e5m2": (ml_dtypes.float8_e5m2, 14)}[fmt]
    v = np.moveaxis(np.asarray(x, np.float32).astype(ml_dtypes.bfloat16).astype(np.float64), axis, -1)
    blocks = v.reshape(v.shape[:-1] + (-1, 32))
    amax = np.abs(blocks).max(-1, keepdims=True)
    byte = np.maximum(np.where(amax > 0, np.frexp(amax)[1] - 1 + 127, 0) - down, 1)
    scale = np.exp2(byte - 127.0)
    codes = (blocks / scale).astype(np.float32).astype(dtype).astype(np.float64)
    return np.moveaxis((codes * scale).reshape(v.shape), -1, axis)


WIDE = False


def mx_kscale(k):
    if not WIDE:
        return np.ones(k)
    levels = np.array([10, -10, 5, -5, 0])
    a = np.random.permutation(np.resize(levels, k // 512 * 4)).reshape(k // 512, 4)
    idx = np.arange(k)
    return np.exp2(a[idx // 512, idx % 128 // 32])


BF16 = ml_dtypes.bfloat16


def bf(x):
    return np.asarray(x, np.float32).astype(BF16)


def f64(x):
    return np.asarray(x).astype(np.float64)


E2M1 = np.array([0.0, 0.5, 1.0, 1.5, 2.0, 3.0, 4.0, 6.0, -0.0, -0.5, -1.0, -1.5, -2.0, -3.0, -4.0, -6.0])


def pack_weight(w, fmt):
    k, n = w.shape
    w = f64(bf(w)).reshape(k // 32, 32, n)
    amax = np.abs(w).max(1)
    if fmt == "e4m3":
        byte = np.frexp(amax)[1] - 1 + 127 - 7
    else:
        mant, ex = np.frexp(amax / 6.0)
        byte = np.where(mant > 0.5, ex, ex - 1) + 127
    byte = np.clip(np.where(amax > 0, byte, 1), 1, 254)
    scaled = (w * np.exp2(127.0 - byte)[:, None, :]).reshape(k, n).astype(np.float32)
    by_word = np.ascontiguousarray(scaled.reshape(k // 512, 128, 4, n).transpose(0, 1, 3, 2))
    if fmt == "e4m3":
        words = by_word.astype(ml_dtypes.float8_e4m3fn).view(np.uint8)
    else:
        c = by_word.astype(ml_dtypes.float4_e2m1fn).view(np.uint8) & 0xF
        words = c[..., 0::2] | (c[..., 1::2] << 4)
    return np.ascontiguousarray(words), np.ascontiguousarray(byte.astype(np.uint8).reshape(k // 512, 16, n))


def unpack_weight(words, scales, fmt):
    g, p, n, _ = words.shape
    if fmt == "e4m3":
        vals = np.ascontiguousarray(words).view(ml_dtypes.float8_e4m3fn).astype(np.float64)
    else:
        nib = np.empty((g, p, n, 4), np.uint8)
        nib[..., 0::2] = words & 0xF
        nib[..., 1::2] = words >> 4
        vals = E2M1[nib]
    vals = vals * np.repeat(np.exp2(scales.astype(np.float64) - 127.0), 8, axis=1)[..., None]
    return vals.transpose(0, 1, 3, 2).reshape(g * 512, n)

def pack4(w):
    words, scales = pack_weight(w, "e2m1")
    return words.reshape(words.shape[0], 128, -1), scales


def unpack4(words, scales):
    return unpack_weight(words.reshape(words.shape[0], 128, -1, 2), scales, "e2m1")


B, Q_LEN, CTX, HID, H, KVH, D = 4, 128, 1408, 1024, 4, 2, 128
T = CTX + Q_LEN
EPS = 1e-6
ROPE_BASE = 10000.0


def rms_norm(x, w):
    return x * (1.0 / np.sqrt(np.mean(x * x, axis=-1, keepdims=True) + EPS)) * w


def rotate_half(x):
    h = x.shape[-1] // 2
    return np.concatenate([-x[..., h:], x[..., :h]], axis=-1)


def setup_inputs():
    s = mx_kscale(HID)
    inv_freq = 1.0 / ROPE_BASE ** (np.arange(0, D, 2) / D)
    pos = np.random.randint(0, CTX, size=(B, 1)) + np.arange(T)[None, :]
    ang = pos[:, :, None] * inv_freq
    emb = np.concatenate([ang, ang], axis=-1)
    hidden_states = bf(np.random.standard_normal((B, Q_LEN, HID)) * s)
    target_hidden = bf(np.random.standard_normal((B, CTX, HID)) * s)
    Wq_words, Wq_scales = pack4((np.random.standard_normal((H * D, HID)) / np.sqrt(HID) / s[None, :]).T)
    Wk_words, Wk_scales = pack4((np.random.standard_normal((KVH * D, HID)) / np.sqrt(HID) / s[None, :]).T)
    Wv_words, Wv_scales = pack4((np.random.standard_normal((KVH * D, HID)) * 2.0 / np.sqrt(HID) / s[None, :]).T)
    return {"hidden_states": hidden_states,
            "target_hidden": target_hidden,
            "cos": bf(np.cos(emb)),
            "sin": bf(np.sin(emb)),
            "Wq_words": Wq_words,
            "Wq_scales": Wq_scales,
            "Wk_words": Wk_words,
            "Wk_scales": Wk_scales,
            "Wv_words": Wv_words,
            "Wv_scales": Wv_scales,
            "q_norm_w": bf(1.0 + 0.1 * np.random.standard_normal(D)),
            "k_norm_w": bf(1.0 + 0.1 * np.random.standard_normal(D))}


def reference(hidden_states, target_hidden, cos, sin, Wq_words, Wq_scales, Wk_words, Wk_scales, Wv_words, Wv_scales, q_norm_w, k_norm_w):
    kv_in = mxq(np.concatenate([f64(target_hidden), f64(hidden_states)], axis=1), 2, "e4m3")
    h_in = kv_in[:, CTX:, :]
    q = (h_in @ unpack4(Wq_words, Wq_scales)).reshape(B, Q_LEN, H, D)
    q = rms_norm(q, f64(q_norm_w)).transpose(0, 2, 1, 3)
    k = (kv_in @ unpack4(Wk_words, Wk_scales)).reshape(B, T, KVH, D)
    k = rms_norm(k, f64(k_norm_w)).transpose(0, 2, 1, 3)
    v = (kv_in @ unpack4(Wv_words, Wv_scales)).reshape(B, T, KVH, D).transpose(0, 2, 1, 3)
    c = f64(cos)[:, None, :, :]
    s = f64(sin)[:, None, :, :]
    q = q * c[:, :, -Q_LEN:, :] + rotate_half(q) * s[:, :, -Q_LEN:, :]
    k = k * c + rotate_half(k) * s
    return q, k, v

@@ -1,0 +1,357 @@
+from contextlib import ExitStack
+
+import concourse.masks as masks
+import concourse.mybir as mybir
+
+F32 = mybir.dt.float32
+BF16 = mybir.dt.bfloat16
+I32 = mybir.dt.int32
+U32 = mybir.dt.uint32
+U8 = mybir.dt.uint8
+FP8X4 = mybir.dt.float8_e4m3fn_x4
+FP4X4 = mybir.dt.float4_e2m1fn_x4
+ACT = mybir.ActivationFunctionType
+ALU = mybir.AluOpType
+
+B, Q_LEN, CTX, HID, H, KVH, D = 4, 128, 1408, 1024, 4, 2, 128
+T = CTX + Q_LEN
+EPS = 1e-6
+HALF = D // 2
+
+P = 128
+PACK = 4
+K_PASS = P * PACK
+PASSES = HID // K_PASS
+WORDS = HID // 2
+N_BANK = 512
+J = CTX // P
+CHUNK = 4
+LOAD_AHEAD = 26
+TABLE_AHEAD = 4
+
+FLOPS = 2 * HID * (B * Q_LEN * H * D + 2 * B * T * KVH * D)
+
+
+def tile_dflashattention_pa_t_kernel(
+    tc,
+    hidden_states,
+    target_hidden,
+    cos,
+    sin,
+    Wq_words,
+    Wq_scales,
+    Wk_words,
+    Wk_scales,
+    Wv_words,
+    Wv_scales,
+    q_norm_w,
+    k_norm_w,
+    out_q,
+    out_k,
+    out_v,
+):
+    nc = tc.nc
+    with ExitStack() as ctx:
+        const = ctx.enter_context(tc.tile_pool(name="const", bufs=1))
+        x_pool = ctx.enter_context(tc.tile_pool(name="x", bufs=1))
+        tab_pool = ctx.enter_context(tc.tile_pool(name="tab", bufs=5))
+        mx_pool = ctx.enter_context(tc.tile_pool(name="mx", bufs=2))
+        rope_pool = ctx.enter_context(tc.tile_pool(name="rope", bufs=2))
+        stat_pool = ctx.enter_context(tc.tile_pool(name="stat", bufs=3))
+        out_pool = ctx.enter_context(tc.tile_pool(name="out", bufs=6))
+        hid_pool = ctx.enter_context(tc.tile_pool(name="hid", bufs=B))
+        xt_psum = ctx.enter_context(tc.psum_pool(name="xt", bufs=4))
+        acc_psum = ctx.enter_context(tc.psum_pool(name="acc", bufs=4))
+        ctx.enter_context(tc.manual_schedule())
+
+        ident = const.tile([P, P], F32, name="ident")
+        masks.make_identity(nc, ident[:])
+        eps = const.tile([P, 1], F32, name="eps")
+        nc.vector.memset(eps[:], EPS)
+        warm = const.tile([P, 1], F32, name="warm")
+        nc.scalar.activation(out=warm[:], in_=eps[:], func=ACT.Sqrt)
+
+        w_kv = const.tile([P, PASSES, 2 * N_BANK], U8, name="w_kv", align_bytes=64)
+        s_kv = const.tile([P, PASSES, N_BANK], U8, name="s_kv", align_bytes=64)
+        w_q = const.tile([P, PASSES, 2 * N_BANK], U8, name="w_q", align_bytes=64)
+        s_q = const.tile([P, PASSES, N_BANK], U8, name="s_q", align_bytes=64)
+        nc.vector.memset(s_kv[:].bitcast(I32), 0)
+        nc.vector.memset(s_q[:].bitcast(I32), 0)
+
+        def load_weight(words, scales, w_tile, s_tile, col0, cols):
+            nc.sync.dma_start(
+                out=w_tile[:, :, 2 * col0 : 2 * (col0 + cols)].bitcast(I32),
+                in_=words.bitcast(I32).rearrange("g p n -> p g n"),
+            )
+            for quad in range(4):
+                nc.sync.dma_start(
+                    out=s_tile[32 * quad : 32 * quad + 4, :, col0 : col0 + cols].bitcast(I32),
+                    in_=scales.bitcast(I32)[:, 4 * quad : 4 * quad + 4, :].rearrange("g r n -> r g n"),
+                )
+
+        norm_w = const.tile([P, 2, D], BF16, name="norm_w")
+        cos_ctx = const.tile([P, B * J, D], BF16, name="cos_ctx")
+        sin_ctx = const.tile([P, B * J, D], BF16, name="sin_ctx")
+        cos_new = const.tile([P, B, D], BF16, name="cos_new")
+        sin_new = const.tile([P, B, D], BF16, name="sin_new")
+
+        def load_norm_weights():
+            nc.gpsimd.dma_start(out=norm_w[:, 0, :], in_=k_norm_w.partition_broadcast(P))
+            nc.gpsimd.dma_start(out=norm_w[:, 1, :], in_=q_norm_w.partition_broadcast(P))
+
+        def load_ctx_tables(b):
+            for table, dst in ((cos, cos_ctx), (sin, sin_ctx)):
+                nc.gpsimd.dma_start(
+                    out=dst[:, b * J : (b + 1) * J, :],
+                    in_=table[b, 0:CTX, :].rearrange("(p j) d -> p j d", j=J),
+                )
+
+        def load_new_tables():
+            for table, dst in ((cos, cos_new), (sin, sin_new)):
+                nc.gpsimd.dma_start(out=dst[:], in_=table[:, CTX:T, :].rearrange("b t d -> t b d"))
+
+        pairs = B * J // 2
+        steps = (
+            [("ctx", m) for m in range(pairs // 2)]
+            + [("new", b) for b in range(B)]
+            + [("ctx", m) for m in range(pairs // 2, pairs)]
+        )
+        n_steps = len(steps)
+        ctx_x = target_hidden.rearrange("b (p j) k -> b p j k", j=J)
+
+        x_tiles = {}
+        xt_banks = {}
+        grouped = {}
+        x_codes = {}
+        acc_banks = {}
+        tables = {}
+        products = {}
+        out_tiles = {}
+
+        def load_tables_for(s):
+            kind, i = steps[s]
+            if kind == "new":
+                if i == 0:
+                    load_new_tables()
+            else:
+                for n in (2 * i, 2 * i + 1):
+                    if n % J == 0:
+                        load_ctx_tables(n // J)
+
+        def load_x(s):
+            kind, i = steps[s]
+            if kind == "new":
+                if i == 0:
+                    load_weight(Wq_words, Wq_scales, w_q, s_q, 0, H * D)
+                x_sb = x_pool.tile([P, 1, HID], BF16, name="x_new%d" % i)
+                nc.sync.dma_start(out=x_sb[:, 0, :], in_=hidden_states[i])
+                x_tiles[s] = [x_sb[:, 0, :].bitcast(F32)]
+            else:
+                x_sb = x_pool.tile([P, 2, HID], BF16, name="x_ctx%d" % i)
+                b0, j0 = divmod(2 * i, J)
+                b1, j1 = divmod(2 * i + 1, J)
+                if b0 == b1:
+                    nc.sync.dma_start(out=x_sb[:], in_=ctx_x[b0, :, j0 : j0 + 2, :])
+                else:
+                    nc.sync.dma_start(out=x_sb[:, 0, :], in_=ctx_x[b0, :, j0, :])
+                    nc.sync.dma_start(out=x_sb[:, 1, :], in_=ctx_x[b1, :, j1, :])
+                x_tiles[s] = [x_sb[:, 0, :].bitcast(F32), x_sb[:, 1, :].bitcast(F32)]
+
+        def make_tables(s):
+            kind, i = steps[s]
+            if kind == "new":
+                c = cos_new[:, i : i + 1, :].to_broadcast([P, 2, D])
+                sn = sin_new[:, i : i + 1, :].to_broadcast([P, 2, D])
+                w = norm_w[:]
+            else:
+                c = cos_ctx[:, 2 * i : 2 * i + 2, :]
+                sn = sin_ctx[:, 2 * i : 2 * i + 2, :]
+                w = norm_w[:, 0:1, :].to_broadcast([P, 2, D])
+            tab = tab_pool.tile([P, 2, 2, D], F32, name="tab", tag="tab")
+            nc.gpsimd.tensor_tensor(out=tab[:, :, 0, :], in0=c, in1=w, op=ALU.mult)
+            nc.gpsimd.tensor_tensor(
+                out=tab[:, :, 1, 0:HALF], in0=sn[:, :, HALF:D], in1=w[:, :, 0:HALF], op=ALU.mult
+            )
+            nc.gpsimd.tensor_tensor(
+                out=tab[:, :, 1, HALF:D], in0=sn[:, :, 0:HALF], in1=w[:, :, HALF:D], op=ALU.mult
+            )
+            tables[s] = tab
+
+        def transpose_x(s):
+            xt_banks[s] = []
+            for words in x_tiles[s]:
+                xt = xt_psum.tile([P, PASSES, 2, P], F32, name="xt", tag="xt")
+                for g in range(PASSES):
+                    for u in range(2):
+                        nc.tensor.transpose(
+                            out=xt[:, g, u, :],
+                            in_=words[:, g * (WORDS // PASSES) + u : (g + 1) * (WORDS // PASSES) : 2],
+                            identity=ident[:],
+                        )
+                xt_banks[s].append(xt)
+
+        def regroup_x(s):
+            grp = mx_pool.tile([P, 2 * PASSES * P * PACK], BF16, name="grp", tag="grp", align_bytes=64)
+            grp_words = grp[:].bitcast(F32).rearrange("p (t g r u) -> p t g r u", t=2, g=PASSES, u=2)
+            for t, xt in enumerate(xt_banks[s]):
+                nc.scalar.copy(out=grp_words[:, t], in_=xt[:].rearrange("p g u r -> p g r u"))
+            grouped[s] = grp
+
+        def quantise_x(s):
+            cols = len(x_tiles[s]) * PASSES * P
+            codes = mx_pool.tile([P, 2 * PASSES * P], U32, name="codes", tag="codes", align_bytes=64)
+            plane = mx_pool.tile([P, 2 * PASSES * P], U8, name="plane", tag="plane", align_bytes=64)
+            nc.vector.quantize_mx(
+                out=codes[:, 0:cols].bitcast(FP8X4),
+                scales=plane[:, 0:cols],
+                in_=grouped[s][:, 0 : cols * PACK],
+            )
+            x_codes[s] = (codes, plane)
+
+        def banks_of(s):
+            if steps[s][0] == "new":
+                return [(0, w_kv, s_kv, KVH, 0), (0, w_q, s_q, H, KVH)]
+            return [(0, w_kv, s_kv, KVH, 0), (1, w_kv, s_kv, KVH, KVH)]
+
+        def project(s):
+            codes, plane = x_codes[s]
+            acc_banks[s] = []
+            for t, w_tile, s_tile, heads, slot in banks_of(s):
+                acc = acc_psum.tile([P, N_BANK], F32, name="acc", tag="acc")
+                for g in range(PASSES):
+                    cols = slice((t * PASSES + g) * P, (t * PASSES + g + 1) * P)
+                    nc.tensor.matmul_mx(
+                        out=acc[:],
+                        lhsT=codes[:, cols].bitcast(FP8X4),
+                        lhsT_scale=plane[:, cols],
+                        rhs=w_tile[:, g, :].bitcast(FP4X4),
+                        rhs_scale=s_tile[:, g, :],
+                        start=(g == 0),
+                        stop=(g == PASSES - 1),
+                    )
+                acc_banks[s].append(acc)
+
+        def destinations(s):
+            kind, i = steps[s]
+            if kind == "new":
+                if s not in out_tiles:
+                    out_tiles[s] = hid_pool.tile([P, 2 * KVH + H, D], F32, name="o_new", tag="o_new")
+                o = out_tiles[s]
+                return [(o[:, 0:KVH, :], o[:, KVH : 2 * KVH, :]), (o[:, 2 * KVH :, :], None)]
+            dst = []
+            for n in (2 * i, 2 * i + 1):
+                b, j = divmod(n, J)
+                c, jj = divmod(j, CHUNK)
+                if (b, c) not in out_tiles:
+                    out_tiles[(b, c)] = out_pool.tile([P, 2, KVH, CHUNK, D], F32, name="o_ctx", tag="o_ctx")
+                o = out_tiles[(b, c)]
+                dst.append((o[:, 0, :, jj, :], o[:, 1, :, jj, :]))
+            return dst
+
+        def sum_squares(s):
+            squares = rope_pool.tile([P, KVH + H, D], BF16, name="squares", tag="squares")
+            sums = stat_pool.tile([P, KVH + H], F32, name="sums", tag="sums")
+            for acc, (t, w_tile, s_tile, heads, slot) in zip(acc_banks[s], banks_of(s)):
+                for h in range(heads):
+                    nc.scalar.activation(
+                        out=squares[:, slot + h, :],
+                        in_=acc[:, h * D : (h + 1) * D],
+                        func=ACT.Square,
+                        accum_out=sums[:, slot + h : slot + h + 1],
+                    )
+            return sums
+
+        def root_mean(s, sums):
+            n_heads = sum(heads for t, w_tile, s_tile, heads, slot in banks_of(s))
+            rms = stat_pool.tile([P, KVH + H], F32, name="rms", tag="rms")
+            nc.scalar.activation(
+                out=rms[:, 0:n_heads], in_=sums[:, 0:n_heads], func=ACT.Sqrt, bias=eps[:], scale=1.0 / D
+            )
+            return rms[:, 0:n_heads]
+
+        def copy_v(s):
+            for acc, (k_dst, v_dst) in zip(acc_banks[s], destinations(s)):
+                if v_dst is not None:
+                    nc.scalar.copy(
+                        out=v_dst, in_=acc[:, KVH * D : 2 * KVH * D].rearrange("p (h d) -> p h d", h=KVH)
+                    )
+
+        def rotate(s, rms):
+            n_heads = rms.shape[1]
+            inv = stat_pool.tile([P, KVH + H], F32, name="inv", tag="inv")
+            nc.vector.reciprocal(out=inv[:, 0:n_heads], in_=rms)
+            prod = rope_pool.tile([P, KVH + H, 2, D], F32, name="prod", tag="prod")
+            for bank, (acc, (t, w_tile, s_tile, heads, slot)) in enumerate(zip(acc_banks[s], banks_of(s))):
+                for h in range(heads):
+                    nc.vector.scalar_tensor_tensor(
+                        out=prod[:, slot + h, :, :],
+                        in0=acc[:, h * D : (h + 1) * D].unsqueeze(1).to_broadcast([P, 2, D]),
+                        scalar=inv[:, slot + h : slot + h + 1],
+                        in1=tables[s][:, bank, :, :],
+                        op0=ALU.mult,
+                        op1=ALU.mult,
+                    )
+            products[s] = prod
+
+        def add_halves(s):
+            prod = products[s]
+            for (k_dst, v_dst), (t, w_tile, s_tile, heads, slot) in zip(destinations(s), banks_of(s)):
+                mine = prod[:, slot : slot + heads, :, :]
+                nc.vector.tensor_tensor(
+                    out=k_dst[:, :, 0:HALF], in0=mine[:, :, 0, 0:HALF], in1=mine[:, :, 1, HALF:D], op=ALU.subtract
+                )
+                nc.vector.tensor_tensor(
+                    out=k_dst[:, :, HALF:D], in0=mine[:, :, 0, HALF:D], in1=mine[:, :, 1, 0:HALF], op=ALU.add
+                )
+
+        def store(s):
+            kind, i = steps[s]
+            if kind == "new":
+                o = out_tiles[s]
+                nc.sync.dma_start(out=out_k[i, :, CTX:T, :].rearrange("h t d -> t h d"), in_=o[:, 0:KVH, :])
+                nc.sync.dma_start(out=out_v[i, :, CTX:T, :].rearrange("h t d -> t h d"), in_=o[:, KVH : 2 * KVH, :])
+                nc.sync.dma_start(out=out_q[i].rearrange("h t d -> t h d"), in_=o[:, 2 * KVH :, :])
+                return
+            for n in (2 * i, 2 * i + 1):
+                b, j = divmod(n, J)
+                c = j // CHUNK
+                first, last = c * CHUNK, min(J, (c + 1) * CHUNK)
+                if j == last - 1:
+                    o = out_tiles[(b, c)]
+                    for which, out in enumerate((out_k, out_v)):
+                        nc.sync.dma_start(
+                            out=out[b, :, 0:CTX, :].rearrange("h (p j) d -> p h j d", j=J)[:, :, first:last, :],
+                            in_=o[:, which, :, 0 : last - first, :],
+                        )
+
+        load_norm_weights()
+        for s in range(TABLE_AHEAD):
+            load_tables_for(s)
+        load_x(0)
+        load_weight(Wk_words, Wk_scales, w_kv, s_kv, 0, KVH * D)
+        load_weight(Wv_words, Wv_scales, w_kv, s_kv, KVH * D, KVH * D)
+        for s in range(1, LOAD_AHEAD):
+            load_x(s)
+
+        for i in range(n_steps + 4):
+            if i + LOAD_AHEAD < n_steps:
+                load_x(i + LOAD_AHEAD)
+            if i + TABLE_AHEAD < n_steps:
+                load_tables_for(i + TABLE_AHEAD)
+            if i < n_steps:
+                make_tables(i)
+                transpose_x(i)
+            if 0 <= i - 2 < n_steps:
+                quantise_x(i - 2)
+                project(i - 2)
+            if 0 <= i - 4 < n_steps:
+                add_halves(i - 4)
+                store(i - 4)
+            if 0 <= i - 3 < n_steps:
+                sums = sum_squares(i - 3)
+                copy_v(i - 3)
+                rms = root_mean(i - 3, sums)
+            if 0 <= i - 1 < n_steps:
+                regroup_x(i - 1)
+            if 0 <= i - 3 < n_steps:
+                rotate(i - 3, rms)

@@ -27,7 +27,6 @@ N_BANK = 512
 J = CTX // P
 CHUNK = 4
 LOAD_AHEAD = 26
-TABLE_AHEAD = 4
 
 FLOPS = 2 * HID * (B * Q_LEN * H * D + 2 * B * T * KVH * D)
 
@@ -54,7 +53,7 @@ def tile_dflashattention_pa_t_kernel(
     with ExitStack() as ctx:
         const = ctx.enter_context(tc.tile_pool(name="const", bufs=1))
         x_pool = ctx.enter_context(tc.tile_pool(name="x", bufs=1))
-        tab_pool = ctx.enter_context(tc.tile_pool(name="tab", bufs=5))
+        tab_pool = ctx.enter_context(tc.tile_pool(name="tab", bufs=2))
         mx_pool = ctx.enter_context(tc.tile_pool(name="mx", bufs=2))
         rope_pool = ctx.enter_context(tc.tile_pool(name="rope", bufs=2))
         stat_pool = ctx.enter_context(tc.tile_pool(name="stat", bufs=3))
@@ -96,19 +95,19 @@ def tile_dflashattention_pa_t_kernel(
         sin_new = const.tile([P, B, D], BF16, name="sin_new")
 
         def load_norm_weights():
-            nc.gpsimd.dma_start(out=norm_w[:, 0, :], in_=k_norm_w.partition_broadcast(P))
-            nc.gpsimd.dma_start(out=norm_w[:, 1, :], in_=q_norm_w.partition_broadcast(P))
+            nc.sync.dma_start(out=norm_w[:, 0, :], in_=k_norm_w.partition_broadcast(P))
+            nc.sync.dma_start(out=norm_w[:, 1, :], in_=q_norm_w.partition_broadcast(P))
 
         def load_ctx_tables(b):
             for table, dst in ((cos, cos_ctx), (sin, sin_ctx)):
-                nc.gpsimd.dma_start(
+                nc.sync.dma_start(
                     out=dst[:, b * J : (b + 1) * J, :],
                     in_=table[b, 0:CTX, :].rearrange("(p j) d -> p j d", j=J),
                 )
 
         def load_new_tables():
             for table, dst in ((cos, cos_new), (sin, sin_new)):
-                nc.gpsimd.dma_start(out=dst[:], in_=table[:, CTX:T, :].rearrange("b t d -> t b d"))
+                nc.sync.dma_start(out=dst[:], in_=table[:, CTX:T, :].rearrange("b t d -> t b d"))
 
         pairs = B * J // 2
         steps = (
@@ -168,11 +167,11 @@ def tile_dflashattention_pa_t_kernel(
                 sn = sin_ctx[:, 2 * i : 2 * i + 2, :]
                 w = norm_w[:, 0:1, :].to_broadcast([P, 2, D])
             tab = tab_pool.tile([P, 2, 2, D], F32, name="tab", tag="tab")
-            nc.gpsimd.tensor_tensor(out=tab[:, :, 0, :], in0=c, in1=w, op=ALU.mult)
-            nc.gpsimd.tensor_tensor(
+            nc.vector.tensor_tensor(out=tab[:, :, 0, :], in0=c, in1=w, op=ALU.mult)
+            nc.vector.tensor_tensor(
                 out=tab[:, :, 1, 0:HALF], in0=sn[:, :, HALF:D], in1=w[:, :, 0:HALF], op=ALU.mult
             )
-            nc.gpsimd.tensor_tensor(
+            nc.vector.tensor_tensor(
                 out=tab[:, :, 1, HALF:D], in0=sn[:, :, 0:HALF], in1=w[:, :, HALF:D], op=ALU.mult
             )
             tables[s] = tab
@@ -324,22 +323,20 @@ def tile_dflashattention_pa_t_kernel(
                             in_=o[:, which, :, 0 : last - first, :],
                         )
 
-        load_norm_weights()
-        for s in range(TABLE_AHEAD):
-            load_tables_for(s)
         load_x(0)
         load_weight(Wk_words, Wk_scales, w_kv, s_kv, 0, KVH * D)
         load_weight(Wv_words, Wv_scales, w_kv, s_kv, KVH * D, KVH * D)
+        load_norm_weights()
+        load_tables_for(0)
         for s in range(1, LOAD_AHEAD):
             load_x(s)
+            load_tables_for(s)
 
         for i in range(n_steps + 4):
             if i + LOAD_AHEAD < n_steps:
                 load_x(i + LOAD_AHEAD)
-            if i + TABLE_AHEAD < n_steps:
-                load_tables_for(i + TABLE_AHEAD)
+                load_tables_for(i + LOAD_AHEAD)
             if i < n_steps:
-                make_tables(i)
                 transpose_x(i)
             if 0 <= i - 2 < n_steps:
                 quantise_x(i - 2)
@@ -354,4 +351,5 @@ def tile_dflashattention_pa_t_kernel(
             if 0 <= i - 1 < n_steps:
                 regroup_x(i - 1)
             if 0 <= i - 3 < n_steps:
+                make_tables(i - 3)
                 rotate(i - 3, rms)

@@ -27,6 +27,7 @@ N_BANK = 512
 J = CTX // P
 CHUNK = 4
 LOAD_AHEAD = 26
+CTX_STEPS_FIRST = 10
 
 FLOPS = 2 * HID * (B * Q_LEN * H * D + 2 * B * T * KVH * D)
 
@@ -53,7 +54,7 @@ def tile_dflashattention_pa_t_kernel(
     with ExitStack() as ctx:
         const = ctx.enter_context(tc.tile_pool(name="const", bufs=1))
         x_pool = ctx.enter_context(tc.tile_pool(name="x", bufs=1))
-        tab_pool = ctx.enter_context(tc.tile_pool(name="tab", bufs=2))
+        tab_pool = ctx.enter_context(tc.tile_pool(name="tab", bufs=3))
         mx_pool = ctx.enter_context(tc.tile_pool(name="mx", bufs=2))
         rope_pool = ctx.enter_context(tc.tile_pool(name="rope", bufs=2))
         stat_pool = ctx.enter_context(tc.tile_pool(name="stat", bufs=3))
@@ -68,7 +69,7 @@ def tile_dflashattention_pa_t_kernel(
         eps = const.tile([P, 1], F32, name="eps")
         nc.vector.memset(eps[:], EPS)
         warm = const.tile([P, 1], F32, name="warm")
-        nc.scalar.activation(out=warm[:], in_=eps[:], func=ACT.Sqrt)
+        nc.scalar.activation(out=warm[:], in_=eps[:], func=ACT.Abs_reciprocal_sqrt)
 
         w_kv = const.tile([P, PASSES, 2 * N_BANK], U8, name="w_kv", align_bytes=64)
         s_kv = const.tile([P, PASSES, N_BANK], U8, name="s_kv", align_bytes=64)
@@ -111,9 +112,9 @@ def tile_dflashattention_pa_t_kernel(
 
         pairs = B * J // 2
         steps = (
-            [("ctx", m) for m in range(pairs // 2)]
+            [("ctx", m) for m in range(CTX_STEPS_FIRST)]
             + [("new", b) for b in range(B)]
-            + [("ctx", m) for m in range(pairs // 2, pairs)]
+            + [("ctx", m) for m in range(CTX_STEPS_FIRST, pairs)]
         )
         n_steps = len(steps)
         ctx_x = target_hidden.rearrange("b (p j) k -> b p j k", j=J)
@@ -158,23 +159,25 @@ def tile_dflashattention_pa_t_kernel(
 
         def make_tables(s):
             kind, i = steps[s]
+            shape = [P, 2, 2, D]
             if kind == "new":
-                c = cos_new[:, i : i + 1, :].to_broadcast([P, 2, D])
-                sn = sin_new[:, i : i + 1, :].to_broadcast([P, 2, D])
-                w = norm_w[:]
+                c = cos_new[:, i : i + 2, :].unsqueeze(2).to_broadcast(shape)
+                sn = sin_new[:, i : i + 2, :].unsqueeze(2).to_broadcast(shape)
+                w = norm_w[:].unsqueeze(1).to_broadcast(shape)
             else:
-                c = cos_ctx[:, 2 * i : 2 * i + 2, :]
-                sn = sin_ctx[:, 2 * i : 2 * i + 2, :]
-                w = norm_w[:, 0:1, :].to_broadcast([P, 2, D])
-            tab = tab_pool.tile([P, 2, 2, D], F32, name="tab", tag="tab")
-            nc.vector.tensor_tensor(out=tab[:, :, 0, :], in0=c, in1=w, op=ALU.mult)
-            nc.vector.tensor_tensor(
-                out=tab[:, :, 1, 0:HALF], in0=sn[:, :, HALF:D], in1=w[:, :, 0:HALF], op=ALU.mult
+                c = cos_ctx[:, 2 * i : 2 * i + 4, :].rearrange("p (s t) d -> p s t d", s=2)
+                sn = sin_ctx[:, 2 * i : 2 * i + 4, :].rearrange("p (s t) d -> p s t d", s=2)
+                w = norm_w[:, 0:1, :].unsqueeze(1).to_broadcast(shape)
+            tab = tab_pool.tile([P, 2, 2, 2, D], F32, name="tab", tag="tab")
+            nc.gpsimd.tensor_tensor(out=tab[:, :, :, 0, :], in0=c, in1=w, op=ALU.mult)
+            nc.gpsimd.tensor_tensor(
+                out=tab[:, :, :, 1, 0:HALF], in0=sn[:, :, :, HALF:D], in1=w[:, :, :, 0:HALF], op=ALU.mult
             )
-            nc.vector.tensor_tensor(
-                out=tab[:, :, 1, HALF:D], in0=sn[:, :, 0:HALF], in1=w[:, :, HALF:D], op=ALU.mult
+            nc.gpsimd.tensor_tensor(
+                out=tab[:, :, :, 1, HALF:D], in0=sn[:, :, :, 0:HALF], in1=w[:, :, :, HALF:D], op=ALU.mult
             )
-            tables[s] = tab
+            tables[s] = tab[:, 0]
+            tables[s + 1] = tab[:, 1]
 
         def transpose_x(s):
             xt_banks[s] = []
@@ -230,22 +233,15 @@ def tile_dflashattention_pa_t_kernel(
                     )
                 acc_banks[s].append(acc)
 
-        def destinations(s):
+        def out_tile_of(s):
             kind, i = steps[s]
-            if kind == "new":
-                if s not in out_tiles:
-                    out_tiles[s] = hid_pool.tile([P, 2 * KVH + H, D], F32, name="o_new", tag="o_new")
-                o = out_tiles[s]
-                return [(o[:, 0:KVH, :], o[:, KVH : 2 * KVH, :]), (o[:, 2 * KVH :, :], None)]
-            dst = []
-            for n in (2 * i, 2 * i + 1):
-                b, j = divmod(n, J)
-                c, jj = divmod(j, CHUNK)
-                if (b, c) not in out_tiles:
-                    out_tiles[(b, c)] = out_pool.tile([P, 2, KVH, CHUNK, D], F32, name="o_ctx", tag="o_ctx")
-                o = out_tiles[(b, c)]
-                dst.append((o[:, 0, :, jj, :], o[:, 1, :, jj, :]))
-            return dst
+            key = s if kind == "new" else ("ctx", 2 * i // CHUNK)
+            if key not in out_tiles:
+                if kind == "new":
+                    out_tiles[key] = hid_pool.tile([P, KVH + H + KVH, D], F32, name="o_new", tag="o_new")
+                else:
+                    out_tiles[key] = out_pool.tile([P, 2, KVH, CHUNK, D], F32, name="o_ctx", tag="o_ctx")
+            return out_tiles[key]
 
         def sum_squares(s):
             squares = rope_pool.tile([P, KVH + H, D], BF16, name="squares", tag="squares")
@@ -260,25 +256,29 @@ def tile_dflashattention_pa_t_kernel(
                     )
             return sums
 
-        def root_mean(s, sums):
+        def inverse_rms(s, sums):
             n_heads = sum(heads for t, w_tile, s_tile, heads, slot in banks_of(s))
-            rms = stat_pool.tile([P, KVH + H], F32, name="rms", tag="rms")
+            inv = stat_pool.tile([P, KVH + H], F32, name="inv", tag="inv")
             nc.scalar.activation(
-                out=rms[:, 0:n_heads], in_=sums[:, 0:n_heads], func=ACT.Sqrt, bias=eps[:], scale=1.0 / D
+                out=inv[:, 0:n_heads],
+                in_=sums[:, 0:n_heads],
+                func=ACT.Abs_reciprocal_sqrt,
+                bias=eps[:],
+                scale=1.0 / D,
             )
-            return rms[:, 0:n_heads]
+            return inv
 
         def copy_v(s):
-            for acc, (k_dst, v_dst) in zip(acc_banks[s], destinations(s)):
-                if v_dst is not None:
-                    nc.scalar.copy(
-                        out=v_dst, in_=acc[:, KVH * D : 2 * KVH * D].rearrange("p (h d) -> p h d", h=KVH)
-                    )
+            kind, i = steps[s]
+            o = out_tile_of(s)
+            if kind == "new":
+                v_dst = [o[:, KVH + H :, :]]
+            else:
+                v_dst = [o[:, 1, :, (2 * i + t) % CHUNK, :] for t in range(2)]
+            for acc, dst in zip(acc_banks[s], v_dst):
+                nc.scalar.copy(out=dst, in_=acc[:, KVH * D : 2 * KVH * D].rearrange("p (h d) -> p h d", h=KVH))
 
-        def rotate(s, rms):
-            n_heads = rms.shape[1]
-            inv = stat_pool.tile([P, KVH + H], F32, name="inv", tag="inv")
-            nc.vector.reciprocal(out=inv[:, 0:n_heads], in_=rms)
+        def rotate(s, inv):
             prod = rope_pool.tile([P, KVH + H, 2, D], F32, name="prod", tag="prod")
             for bank, (acc, (t, w_tile, s_tile, heads, slot)) in enumerate(zip(acc_banks[s], banks_of(s))):
                 for h in range(heads):
@@ -293,35 +293,41 @@ def tile_dflashattention_pa_t_kernel(
             products[s] = prod
 
         def add_halves(s):
-            prod = products[s]
-            for (k_dst, v_dst), (t, w_tile, s_tile, heads, slot) in zip(destinations(s), banks_of(s)):
-                mine = prod[:, slot : slot + heads, :, :]
-                nc.vector.tensor_tensor(
-                    out=k_dst[:, :, 0:HALF], in0=mine[:, :, 0, 0:HALF], in1=mine[:, :, 1, HALF:D], op=ALU.subtract
-                )
-                nc.vector.tensor_tensor(
-                    out=k_dst[:, :, HALF:D], in0=mine[:, :, 0, HALF:D], in1=mine[:, :, 1, 0:HALF], op=ALU.add
-                )
+            kind, i = steps[s]
+            o = out_tile_of(s)
+            if kind == "new":
+                dst = o[:, 0 : KVH + H, :].unsqueeze(1)
+                src = products[s][:].unsqueeze(1)
+            else:
+                first = 2 * i % CHUNK
+                dst = o[:, 0, :, first : first + 2, :]
+                src = products[s][:, 0 : 2 * KVH].rearrange("p (t h) c d -> p h t c d", t=2)
+            nc.vector.tensor_tensor(
+                out=dst[:, :, :, 0:HALF], in0=src[:, :, :, 0, 0:HALF], in1=src[:, :, :, 1, HALF:D], op=ALU.subtract
+            )
+            nc.vector.tensor_tensor(
+                out=dst[:, :, :, HALF:D], in0=src[:, :, :, 0, HALF:D], in1=src[:, :, :, 1, 0:HALF], op=ALU.add
+            )
 
         def store(s):
             kind, i = steps[s]
+            o = out_tile_of(s)
             if kind == "new":
-                o = out_tiles[s]
                 nc.sync.dma_start(out=out_k[i, :, CTX:T, :].rearrange("h t d -> t h d"), in_=o[:, 0:KVH, :])
-                nc.sync.dma_start(out=out_v[i, :, CTX:T, :].rearrange("h t d -> t h d"), in_=o[:, KVH : 2 * KVH, :])
-                nc.sync.dma_start(out=out_q[i].rearrange("h t d -> t h d"), in_=o[:, 2 * KVH :, :])
-                return
-            for n in (2 * i, 2 * i + 1):
-                b, j = divmod(n, J)
-                c = j // CHUNK
-                first, last = c * CHUNK, min(J, (c + 1) * CHUNK)
-                if j == last - 1:
-                    o = out_tiles[(b, c)]
-                    for which, out in enumerate((out_k, out_v)):
-                        nc.sync.dma_start(
-                            out=out[b, :, 0:CTX, :].rearrange("h (p j) d -> p h j d", j=J)[:, :, first:last, :],
-                            in_=o[:, which, :, 0 : last - first, :],
-                        )
+                nc.sync.dma_start(out=out_q[i].rearrange("h t d -> t h d"), in_=o[:, KVH : KVH + H, :])
+                nc.sync.dma_start(out=out_v[i, :, CTX:T, :].rearrange("h t d -> t h d"), in_=o[:, KVH + H :, :])
+            elif (2 * i + 2) % CHUNK == 0:
+                n_last = 2 * i + 2
+                n_first = n_last - CHUNK
+                for b in range(B):
+                    lo, hi = max(n_first, b * J), min(n_last, (b + 1) * J)
+                    if lo < hi:
+                        for which, out in enumerate((out_k, out_v)):
+                            rows = out[b, :, 0:CTX, :].rearrange("h (p j) d -> p h j d", j=J)
+                            nc.sync.dma_start(
+                                out=rows[:, :, lo - b * J : hi - b * J, :],
+                                in_=o[:, which, :, lo - n_first : hi - n_first, :],
+                            )
 
         load_x(0)
         load_weight(Wk_words, Wk_scales, w_kv, s_kv, 0, KVH * D)
@@ -337,6 +343,8 @@ def tile_dflashattention_pa_t_kernel(
                 load_x(i + LOAD_AHEAD)
                 load_tables_for(i + LOAD_AHEAD)
             if i < n_steps:
+                if i % 2 == 0:
+                    make_tables(i)
                 transpose_x(i)
             if 0 <= i - 2 < n_steps:
                 quantise_x(i - 2)
@@ -347,9 +355,8 @@ def tile_dflashattention_pa_t_kernel(
             if 0 <= i - 3 < n_steps:
                 sums = sum_squares(i - 3)
                 copy_v(i - 3)
-                rms = root_mean(i - 3, sums)
+                inv = inverse_rms(i - 3, sums)
             if 0 <= i - 1 < n_steps:
                 regroup_x(i - 1)
             if 0 <= i - 3 < n_steps:
-                make_tables(i - 3)
-                rotate(i - 3, rms)
+                rotate(i - 3, inv)

@@ -27,7 +27,7 @@ N_BANK = 512
 J = CTX // P
 CHUNK = 4
 LOAD_AHEAD = 26
-CTX_STEPS_FIRST = 10
+NEW_AFTER = 8
 
 FLOPS = 2 * HID * (B * Q_LEN * H * D + 2 * B * T * KVH * D)
 
@@ -78,11 +78,13 @@ def tile_dflashattention_pa_t_kernel(
         nc.vector.memset(s_kv[:].bitcast(I32), 0)
         nc.vector.memset(s_q[:].bitcast(I32), 0)
 
-        def load_weight(words, scales, w_tile, s_tile, col0, cols):
+        def load_words(words, w_tile, col0, cols):
             nc.sync.dma_start(
                 out=w_tile[:, :, 2 * col0 : 2 * (col0 + cols)].bitcast(I32),
                 in_=words.bitcast(I32).rearrange("g p n -> p g n"),
             )
+
+        def load_scales(scales, s_tile, col0, cols):
             for quad in range(4):
                 nc.sync.dma_start(
                     out=s_tile[32 * quad : 32 * quad + 4, :, col0 : col0 + cols].bitcast(I32),
@@ -95,13 +97,13 @@ def tile_dflashattention_pa_t_kernel(
         cos_new = const.tile([P, B, D], BF16, name="cos_new")
         sin_new = const.tile([P, B, D], BF16, name="sin_new")
 
-        def load_norm_weights():
-            nc.sync.dma_start(out=norm_w[:, 0, :], in_=k_norm_w.partition_broadcast(P))
-            nc.sync.dma_start(out=norm_w[:, 1, :], in_=q_norm_w.partition_broadcast(P))
+        def load_norm_weights(queue):
+            queue.dma_start(out=norm_w[:, 0, :], in_=k_norm_w.partition_broadcast(P))
+            queue.dma_start(out=norm_w[:, 1, :], in_=q_norm_w.partition_broadcast(P))
 
-        def load_ctx_tables(b):
+        def load_ctx_tables(b, queue):
             for table, dst in ((cos, cos_ctx), (sin, sin_ctx)):
-                nc.sync.dma_start(
+                queue.dma_start(
                     out=dst[:, b * J : (b + 1) * J, :],
                     in_=table[b, 0:CTX, :].rearrange("(p j) d -> p j d", j=J),
                 )
@@ -111,11 +113,14 @@ def tile_dflashattention_pa_t_kernel(
                 nc.sync.dma_start(out=dst[:], in_=table[:, CTX:T, :].rearrange("b t d -> t b d"))
 
         pairs = B * J // 2
-        steps = (
-            [("ctx", m) for m in range(CTX_STEPS_FIRST)]
-            + [("new", b) for b in range(B)]
-            + [("ctx", m) for m in range(CTX_STEPS_FIRST, pairs)]
-        )
+        steps = []
+        for m in range(pairs):
+            steps.append(("ctx", m))
+            if (m + 1) % NEW_AFTER == 0:
+                b = 2 * ((m + 1) // NEW_AFTER - 1)
+                steps.append(("new", b))
+                steps.append(("new", b + 1))
+        assert len(steps) == pairs + B
         n_steps = len(steps)
         ctx_x = target_hidden.rearrange("b (p j) k -> b p j k", j=J)
 
@@ -136,13 +141,14 @@ def tile_dflashattention_pa_t_kernel(
             else:
                 for n in (2 * i, 2 * i + 1):
                     if n % J == 0:
-                        load_ctx_tables(n // J)
+                        load_ctx_tables(n // J, nc.sync)
 
         def load_x(s):
             kind, i = steps[s]
             if kind == "new":
                 if i == 0:
-                    load_weight(Wq_words, Wq_scales, w_q, s_q, 0, H * D)
+                    load_words(Wq_words, w_q, 0, H * D)
+                    load_scales(Wq_scales, s_q, 0, H * D)
                 x_sb = x_pool.tile([P, 1, HID], BF16, name="x_new%d" % i)
                 nc.sync.dma_start(out=x_sb[:, 0, :], in_=hidden_states[i])
                 x_tiles[s] = [x_sb[:, 0, :].bitcast(F32)]
@@ -309,32 +315,36 @@ def tile_dflashattention_pa_t_kernel(
                 out=dst[:, :, :, HALF:D], in0=src[:, :, :, 0, HALF:D], in1=src[:, :, :, 1, 0:HALF], op=ALU.add
             )
 
-        def store(s):
+        def store(s, which):
             kind, i = steps[s]
             o = out_tile_of(s)
+            out = (out_k, out_v)[which]
             if kind == "new":
-                nc.sync.dma_start(out=out_k[i, :, CTX:T, :].rearrange("h t d -> t h d"), in_=o[:, 0:KVH, :])
-                nc.sync.dma_start(out=out_q[i].rearrange("h t d -> t h d"), in_=o[:, KVH : KVH + H, :])
-                nc.sync.dma_start(out=out_v[i, :, CTX:T, :].rearrange("h t d -> t h d"), in_=o[:, KVH + H :, :])
+                heads = (o[:, 0:KVH, :], o[:, KVH + H :, :])[which]
+                nc.sync.dma_start(out=out[i, :, CTX:T, :].rearrange("h t d -> t h d"), in_=heads)
+                if which == 0:
+                    nc.sync.dma_start(out=out_q[i].rearrange("h t d -> t h d"), in_=o[:, KVH : KVH + H, :])
             elif (2 * i + 2) % CHUNK == 0:
                 n_last = 2 * i + 2
                 n_first = n_last - CHUNK
                 for b in range(B):
                     lo, hi = max(n_first, b * J), min(n_last, (b + 1) * J)
                     if lo < hi:
-                        for which, out in enumerate((out_k, out_v)):
-                            rows = out[b, :, 0:CTX, :].rearrange("h (p j) d -> p h j d", j=J)
-                            nc.sync.dma_start(
-                                out=rows[:, :, lo - b * J : hi - b * J, :],
-                                in_=o[:, which, :, lo - n_first : hi - n_first, :],
-                            )
+                        rows = out[b, :, 0:CTX, :].rearrange("h (p j) d -> p h j d", j=J)
+                        nc.sync.dma_start(
+                            out=rows[:, :, lo - b * J : hi - b * J, :],
+                            in_=o[:, which, :, lo - n_first : hi - n_first, :],
+                        )
 
+        load_norm_weights(nc.gpsimd)
+        load_ctx_tables(0, nc.gpsimd)
         load_x(0)
-        load_weight(Wk_words, Wk_scales, w_kv, s_kv, 0, KVH * D)
-        load_weight(Wv_words, Wv_scales, w_kv, s_kv, KVH * D, KVH * D)
-        load_norm_weights()
-        load_tables_for(0)
-        for s in range(1, LOAD_AHEAD):
+        load_words(Wk_words, w_kv, 0, KVH * D)
+        load_words(Wv_words, w_kv, KVH * D, KVH * D)
+        load_x(1)
+        load_scales(Wk_scales, s_kv, 0, KVH * D)
+        load_scales(Wv_scales, s_kv, KVH * D, KVH * D)
+        for s in range(2, LOAD_AHEAD):
             load_x(s)
             load_tables_for(s)
 
@@ -351,10 +361,11 @@ def tile_dflashattention_pa_t_kernel(
                 project(i - 2)
             if 0 <= i - 4 < n_steps:
                 add_halves(i - 4)
-                store(i - 4)
+                store(i - 4, 0)
             if 0 <= i - 3 < n_steps:
                 sums = sum_squares(i - 3)
                 copy_v(i - 3)
+                store(i - 3, 1)
                 inv = inverse_rms(i - 3, sums)
             if 0 <= i - 1 < n_steps:
                 regroup_x(i - 1)

@@ -56,6 +56,7 @@ def tile_dflashattention_pa_t_kernel(
         x_pool = ctx.enter_context(tc.tile_pool(name="x", bufs=1))
         tab_pool = ctx.enter_context(tc.tile_pool(name="tab", bufs=3))
         mx_pool = ctx.enter_context(tc.tile_pool(name="mx", bufs=2))
+        code_pool = ctx.enter_context(tc.tile_pool(name="code", bufs=3))
         rope_pool = ctx.enter_context(tc.tile_pool(name="rope", bufs=2))
         stat_pool = ctx.enter_context(tc.tile_pool(name="stat", bufs=3))
         out_pool = ctx.enter_context(tc.tile_pool(name="out", bufs=6))
@@ -185,18 +186,17 @@ def tile_dflashattention_pa_t_kernel(
             tables[s] = tab[:, 0]
             tables[s + 1] = tab[:, 1]
 
-        def transpose_x(s):
-            xt_banks[s] = []
-            for words in x_tiles[s]:
-                xt = xt_psum.tile([P, PASSES, 2, P], F32, name="xt", tag="xt")
-                for g in range(PASSES):
-                    for u in range(2):
-                        nc.tensor.transpose(
-                            out=xt[:, g, u, :],
-                            in_=words[:, g * (WORDS // PASSES) + u : (g + 1) * (WORDS // PASSES) : 2],
-                            identity=ident[:],
-                        )
-                xt_banks[s].append(xt)
+        def transpose_x(s, t):
+            words = x_tiles[s][t]
+            xt = xt_psum.tile([P, PASSES, 2, P], F32, name="xt", tag="xt")
+            for g in range(PASSES):
+                for u in range(2):
+                    nc.tensor.transpose(
+                        out=xt[:, g, u, :],
+                        in_=words[:, g * (WORDS // PASSES) + u : (g + 1) * (WORDS // PASSES) : 2],
+                        identity=ident[:],
+                    )
+            xt_banks.setdefault(s, []).append(xt)
 
         def regroup_x(s):
             grp = mx_pool.tile([P, 2 * PASSES * P * PACK], BF16, name="grp", tag="grp", align_bytes=64)
@@ -207,8 +207,8 @@ def tile_dflashattention_pa_t_kernel(
 
         def quantise_x(s):
             cols = len(x_tiles[s]) * PASSES * P
-            codes = mx_pool.tile([P, 2 * PASSES * P], U32, name="codes", tag="codes", align_bytes=64)
-            plane = mx_pool.tile([P, 2 * PASSES * P], U8, name="plane", tag="plane", align_bytes=64)
+            codes = code_pool.tile([P, 2 * PASSES * P], U32, name="codes", tag="codes", align_bytes=64)
+            plane = code_pool.tile([P, 2 * PASSES * P], U8, name="plane", tag="plane", align_bytes=64)
             nc.vector.quantize_mx(
                 out=codes[:, 0:cols].bitcast(FP8X4),
                 scales=plane[:, 0:cols],
@@ -221,23 +221,22 @@ def tile_dflashattention_pa_t_kernel(
                 return [(0, w_kv, s_kv, KVH, 0), (0, w_q, s_q, H, KVH)]
             return [(0, w_kv, s_kv, KVH, 0), (1, w_kv, s_kv, KVH, KVH)]
 
-        def project(s):
+        def project(s, bank):
             codes, plane = x_codes[s]
-            acc_banks[s] = []
-            for t, w_tile, s_tile, heads, slot in banks_of(s):
-                acc = acc_psum.tile([P, N_BANK], F32, name="acc", tag="acc")
-                for g in range(PASSES):
-                    cols = slice((t * PASSES + g) * P, (t * PASSES + g + 1) * P)
-                    nc.tensor.matmul_mx(
-                        out=acc[:],
-                        lhsT=codes[:, cols].bitcast(FP8X4),
-                        lhsT_scale=plane[:, cols],
-                        rhs=w_tile[:, g, :].bitcast(FP4X4),
-                        rhs_scale=s_tile[:, g, :],
-                        start=(g == 0),
-                        stop=(g == PASSES - 1),
-                    )
-                acc_banks[s].append(acc)
+            t, w_tile, s_tile, heads, slot = banks_of(s)[bank]
+            acc = acc_psum.tile([P, N_BANK], F32, name="acc", tag="acc")
+            for g in range(PASSES):
+                cols = slice((t * PASSES + g) * P, (t * PASSES + g + 1) * P)
+                nc.tensor.matmul_mx(
+                    out=acc[:],
+                    lhsT=codes[:, cols].bitcast(FP8X4),
+                    lhsT_scale=plane[:, cols],
+                    rhs=w_tile[:, g, :].bitcast(FP4X4),
+                    rhs_scale=s_tile[:, g, :],
+                    start=(g == 0),
+                    stop=(g == PASSES - 1),
+                )
+            acc_banks.setdefault(s, []).append(acc)
 
         def out_tile_of(s):
             kind, i = steps[s]
@@ -348,26 +347,28 @@ def tile_dflashattention_pa_t_kernel(
             load_x(s)
             load_tables_for(s)
 
-        for i in range(n_steps + 4):
+        for i in range(n_steps + 5):
             if i + LOAD_AHEAD < n_steps:
                 load_x(i + LOAD_AHEAD)
                 load_tables_for(i + LOAD_AHEAD)
-            if i < n_steps:
-                if i % 2 == 0:
-                    make_tables(i)
-                transpose_x(i)
+            if i < n_steps and i % 2 == 0:
+                make_tables(i)
+            for half in range(2):
+                if i < n_steps and half < len(x_tiles[i]):
+                    transpose_x(i, half)
+                if 0 <= i - 3 < n_steps:
+                    project(i - 3, half)
             if 0 <= i - 2 < n_steps:
                 quantise_x(i - 2)
-                project(i - 2)
+            if 0 <= i - 5 < n_steps:
+                add_halves(i - 5)
+                store(i - 5, 0)
             if 0 <= i - 4 < n_steps:
-                add_halves(i - 4)
-                store(i - 4, 0)
-            if 0 <= i - 3 < n_steps:
-                sums = sum_squares(i - 3)
-                copy_v(i - 3)
-                store(i - 3, 1)
-                inv = inverse_rms(i - 3, sums)
+                sums = sum_squares(i - 4)
+                copy_v(i - 4)
+                store(i - 4, 1)
+                inv = inverse_rms(i - 4, sums)
             if 0 <= i - 1 < n_steps:
                 regroup_x(i - 1)
-            if 0 <= i - 3 < n_steps:
-                rotate(i - 3, inv)
+            if 0 <= i - 4 < n_steps:
+                rotate(i - 4, inv)

@@ -56,7 +56,7 @@ def tile_dflashattention_pa_t_kernel(
         x_pool = ctx.enter_context(tc.tile_pool(name="x", bufs=1))
         tab_pool = ctx.enter_context(tc.tile_pool(name="tab", bufs=3))
         mx_pool = ctx.enter_context(tc.tile_pool(name="mx", bufs=2))
-        code_pool = ctx.enter_context(tc.tile_pool(name="code", bufs=3))
+        code_pool = ctx.enter_context(tc.tile_pool(name="code", bufs=4))
         rope_pool = ctx.enter_context(tc.tile_pool(name="rope", bufs=2))
         stat_pool = ctx.enter_context(tc.tile_pool(name="stat", bufs=3))
         out_pool = ctx.enter_context(tc.tile_pool(name="out", bufs=6))
@@ -347,28 +347,43 @@ def tile_dflashattention_pa_t_kernel(
             load_x(s)
             load_tables_for(s)
 
-        for i in range(n_steps + 5):
-            if i + LOAD_AHEAD < n_steps:
-                load_x(i + LOAD_AHEAD)
-                load_tables_for(i + LOAD_AHEAD)
-            if i < n_steps and i % 2 == 0:
-                make_tables(i)
-            for half in range(2):
-                if i < n_steps and half < len(x_tiles[i]):
-                    transpose_x(i, half)
-                if 0 <= i - 3 < n_steps:
-                    project(i - 3, half)
-            if 0 <= i - 2 < n_steps:
-                quantise_x(i - 2)
-            if 0 <= i - 5 < n_steps:
-                add_halves(i - 5)
-                store(i - 5, 0)
-            if 0 <= i - 4 < n_steps:
-                sums = sum_squares(i - 4)
-                copy_v(i - 4)
-                store(i - 4, 1)
-                inv = inverse_rms(i - 4, sums)
-            if 0 <= i - 1 < n_steps:
-                regroup_x(i - 1)
-            if 0 <= i - 4 < n_steps:
-                rotate(i - 4, inv)
+        def live(s):
+            return 0 <= s < n_steps
+
+        def after_projection(s):
+            sums = sum_squares(s)
+            copy_v(s)
+            store(s, 1)
+            inv = inverse_rms(s, sums)
+            rotate(s, inv)
+
+        for r in range(n_steps // 2 + 3):
+            first = 2 * r
+            if live(first):
+                make_tables(first)
+            for s in (first, first + 1):
+                if live(s):
+                    for t in range(len(x_tiles[s])):
+                        transpose_x(s, t)
+            if live(first - 2):
+                project(first - 2, 0)
+                project(first - 2, 1)
+            if live(first - 3):
+                after_projection(first - 3)
+            if live(first - 1):
+                project(first - 1, 0)
+                project(first - 1, 1)
+            if live(first - 4):
+                add_halves(first - 4)
+                store(first - 4, 0)
+            if live(first):
+                regroup_x(first)
+                quantise_x(first)
+            if live(first - 3):
+                add_halves(first - 3)
+                store(first - 3, 0)
+            if live(first + 1):
+                regroup_x(first + 1)
+                quantise_x(first + 1)
+            if live(first - 2):
+                after_projection(first - 2)

@@ -98,9 +98,22 @@ def tile_dflashattention_pa_t_kernel(
         cos_new = const.tile([P, B, D], BF16, name="cos_new")
         sin_new = const.tile([P, B, D], BF16, name="sin_new")
 
-        def load_norm_weights(queue):
-            queue.dma_start(out=norm_w[:, 0, :], in_=k_norm_w.partition_broadcast(P))
-            queue.dma_start(out=norm_w[:, 1, :], in_=q_norm_w.partition_broadcast(P))
+        def load_norm_weights():
+            ones = const.tile([P, P], BF16, name="ones")
+            nc.vector.memset(ones[:], 1.0)
+            w_rows = const.tile([P, 2, D], BF16, name="w_rows")
+            nc.vector.memset(w_rows[:], 0.0)
+            nc.sync.dma_start(out=w_rows[0:1, 0, :], in_=k_norm_w.unsqueeze(0))
+            nc.sync.dma_start(out=w_rows[0:1, 1, :], in_=q_norm_w.unsqueeze(0))
+            spread = acc_psum.tile([P, N_BANK], F32, name="acc", tag="acc")
+            nc.tensor.matmul(
+                out=spread[:, 0 : 2 * D],
+                lhsT=ones[:],
+                rhs=w_rows[:].rearrange("p a d -> p (a d)"),
+                start=True,
+                stop=True,
+            )
+            nc.vector.tensor_copy(out=norm_w[:].rearrange("p a d -> p (a d)"), in_=spread[:, 0 : 2 * D])
 
         def load_ctx_tables(b, queue):
             for table, dst in ((cos, cos_ctx), (sin, sin_ctx)):
@@ -157,7 +170,12 @@ def tile_dflashattention_pa_t_kernel(
                 x_sb = x_pool.tile([P, 2, HID], BF16, name="x_ctx%d" % i)
                 b0, j0 = divmod(2 * i, J)
                 b1, j1 = divmod(2 * i + 1, J)
-                if b0 == b1:
+                if s == 0:
+                    for t in range(2):
+                        for g in range(PASSES):
+                            k_cols = slice(g * K_PASS, (g + 1) * K_PASS)
+                            nc.sync.dma_start(out=x_sb[:, t, k_cols], in_=ctx_x[b0, :, j0 + t, k_cols])
+                elif b0 == b1:
                     nc.sync.dma_start(out=x_sb[:], in_=ctx_x[b0, :, j0 : j0 + 2, :])
                 else:
                     nc.sync.dma_start(out=x_sb[:, 0, :], in_=ctx_x[b0, :, j0, :])
@@ -335,7 +353,7 @@ def tile_dflashattention_pa_t_kernel(
                             in_=o[:, which, :, lo - n_first : hi - n_first, :],
                         )
 
-        load_norm_weights(nc.gpsimd)
+        load_norm_weights()
         load_ctx_tables(0, nc.gpsimd)
         load_x(0)
         load_words(Wk_words, w_kv, 0, KVH * D)

@@ -98,13 +98,16 @@ def tile_dflashattention_pa_t_kernel(
         cos_new = const.tile([P, B, D], BF16, name="cos_new")
         sin_new = const.tile([P, B, D], BF16, name="sin_new")
 
-        def load_norm_weights():
-            ones = const.tile([P, P], BF16, name="ones")
-            nc.vector.memset(ones[:], 1.0)
-            w_rows = const.tile([P, 2, D], BF16, name="w_rows")
-            nc.vector.memset(w_rows[:], 0.0)
+        ones = const.tile([P, P], BF16, name="ones")
+        nc.vector.memset(ones[:], 1.0)
+        w_rows = const.tile([P, 2, D], BF16, name="w_rows")
+        nc.vector.memset(w_rows[:], 0.0)
+
+        def load_norm_rows():
             nc.sync.dma_start(out=w_rows[0:1, 0, :], in_=k_norm_w.unsqueeze(0))
             nc.sync.dma_start(out=w_rows[0:1, 1, :], in_=q_norm_w.unsqueeze(0))
+
+        def spread_norm_weights():
             spread = acc_psum.tile([P, N_BANK], F32, name="acc", tag="acc")
             nc.tensor.matmul(
                 out=spread[:, 0 : 2 * D],
@@ -353,9 +356,9 @@ def tile_dflashattention_pa_t_kernel(
                             in_=o[:, which, :, lo - n_first : hi - n_first, :],
                         )
 
-        load_norm_weights()
         load_ctx_tables(0, nc.gpsimd)
         load_x(0)
+        load_norm_rows()
         load_words(Wk_words, w_kv, 0, KVH * D)
         load_words(Wv_words, w_kv, KVH * D, KVH * D)
         load_x(1)
@@ -375,33 +378,56 @@ def tile_dflashattention_pa_t_kernel(
             inv = inverse_rms(s, sums)
             rotate(s, inv)
 
-        for r in range(n_steps // 2 + 3):
+        def transposes(s):
+            for t in range(len(x_tiles[s])):
+                transpose_x(s, t)
+
+        def prepare(s):
+            regroup_x(s)
+            quantise_x(s)
+
+        def project_step(s):
+            project(s, 0)
+            project(s, 1)
+
+        transposes(0)
+        spread_norm_weights()
+        transposes(1)
+        make_tables(0)
+        prepare(0)
+        project_step(0)
+        prepare(1)
+        after_projection(0)
+        transposes(2)
+        transposes(3)
+        make_tables(2)
+        project_step(1)
+        prepare(2)
+        prepare(3)
+        after_projection(1)
+
+        for r in range(2, n_steps // 2 + 3):
             first = 2 * r
-            if live(first):
-                make_tables(first)
             for s in (first, first + 1):
                 if live(s):
-                    for t in range(len(x_tiles[s])):
-                        transpose_x(s, t)
+                    transposes(s)
+            if live(first):
+                make_tables(first)
             if live(first - 2):
-                project(first - 2, 0)
-                project(first - 2, 1)
-            if live(first - 3):
+                project_step(first - 2)
+            if live(first - 3) and r > 2:
                 after_projection(first - 3)
             if live(first - 1):
-                project(first - 1, 0)
-                project(first - 1, 1)
+                project_step(first - 1)
             if live(first - 4):
                 add_halves(first - 4)
                 store(first - 4, 0)
             if live(first):
-                regroup_x(first)
-                quantise_x(first)
+                prepare(first)
             if live(first - 3):
                 add_halves(first - 3)
                 store(first - 3, 0)
             if live(first + 1):
-                regroup_x(first + 1)
-                quantise_x(first + 1)
+                prepare(first + 1)
             if live(first - 2):
                 after_projection(first - 2)

@@ -27,6 +27,7 @@ N_BANK = 512
 J = CTX // P
 CHUNK = 4
 LOAD_AHEAD = 26
+WARM_UP = 4
 NEW_AFTER = 8
 
 FLOPS = 2 * HID * (B * Q_LEN * H * D + 2 * B * T * KVH * D)
@@ -65,6 +66,10 @@ def tile_dflashattention_pa_t_kernel(
         acc_psum = ctx.enter_context(tc.psum_pool(name="acc", bufs=4))
         ctx.enter_context(tc.manual_schedule())
 
+        ones = const.tile([P, P], BF16, name="ones")
+        nc.vector.memset(ones[:], 1.0)
+        zeros = const.tile([P, N_BANK], BF16, name="zeros")
+        nc.vector.memset(zeros[:], 0.0)
         ident = const.tile([P, P], F32, name="ident")
         masks.make_identity(nc, ident[:])
         eps = const.tile([P, 1], F32, name="eps")
@@ -98,10 +103,13 @@ def tile_dflashattention_pa_t_kernel(
         cos_new = const.tile([P, B, D], BF16, name="cos_new")
         sin_new = const.tile([P, B, D], BF16, name="sin_new")
 
-        ones = const.tile([P, P], BF16, name="ones")
-        nc.vector.memset(ones[:], 1.0)
         w_rows = const.tile([P, 2, D], BF16, name="w_rows")
         nc.vector.memset(w_rows[:], 0.0)
+
+        def warm_up():
+            idle = acc_psum.tile([P, N_BANK], F32, name="acc", tag="acc")
+            for n in range(WARM_UP):
+                nc.tensor.matmul(out=idle[:], lhsT=ones[:], rhs=zeros[:], start=True, stop=True)
 
         def load_norm_rows():
             nc.sync.dma_start(out=w_rows[0:1, 0, :], in_=k_norm_w.unsqueeze(0))
@@ -390,6 +398,7 @@ def tile_dflashattention_pa_t_kernel(
             project(s, 0)
             project(s, 1)
 
+        warm_up()
         transposes(0)
         spread_norm_weights()
         transposes(1)

@@ -206,12 +206,20 @@ def tile_dflashattention_pa_t_kernel(
                 w = norm_w[:, 0:1, :].unsqueeze(1).to_broadcast(shape)
             tab = tab_pool.tile([P, 2, 2, 2, D], F32, name="tab", tag="tab")
             nc.gpsimd.tensor_tensor(out=tab[:, :, :, 0, :], in0=c, in1=w, op=ALU.mult)
-            nc.gpsimd.tensor_tensor(
-                out=tab[:, :, :, 1, 0:HALF], in0=sn[:, :, :, HALF:D], in1=w[:, :, :, 0:HALF], op=ALU.mult
-            )
-            nc.gpsimd.tensor_tensor(
-                out=tab[:, :, :, 1, HALF:D], in0=sn[:, :, :, 0:HALF], in1=w[:, :, :, HALF:D], op=ALU.mult
-            )
+            if kind == "new":
+                nc.gpsimd.tensor_tensor(
+                    out=tab[:, :, :, 1, 0:HALF], in0=sn[:, :, :, HALF:D], in1=w[:, :, :, 0:HALF], op=ALU.mult
+                )
+                nc.gpsimd.tensor_tensor(
+                    out=tab[:, :, :, 1, HALF:D], in0=sn[:, :, :, 0:HALF], in1=w[:, :, :, HALF:D], op=ALU.mult
+                )
+            else:
+                nc.gpsimd.tensor_tensor(
+                    out=tab[:].rearrange("p s t c (a e) -> p (s t) c a e", a=2)[:, :, 1, :, :],
+                    in0=sin_ctx[:, 2 * i : 2 * i + 4, :].rearrange("p n (a e) -> p n a e", a=2)[:, :, ::-1, :],
+                    in1=norm_w[:, 0:1, :].to_broadcast([P, 4, D]).rearrange("p n (a e) -> p n a e", a=2),
+                    op=ALU.mult,
+                )
             tables[s] = tab[:, 0]
             tables[s + 1] = tab[:, 1]
 

@@ -374,10 +374,10 @@ def tile_dflashattention_pa_t_kernel(
 
         load_ctx_tables(0, nc.gpsimd)
         load_x(0)
+        load_x(1)
         load_norm_rows()
         load_words(Wk_words, w_kv, 0, KVH * D)
         load_words(Wv_words, w_kv, KVH * D, KVH * D)
-        load_x(1)
         load_scales(Wk_scales, s_kv, 0, KVH * D)
         load_scales(Wv_scales, s_kv, KVH * D, KVH * D)
         for s in range(2, LOAD_AHEAD):

@@ -61,7 +61,7 @@ def tile_dflashattention_pa_t_kernel(
         rope_pool = ctx.enter_context(tc.tile_pool(name="rope", bufs=2))
         stat_pool = ctx.enter_context(tc.tile_pool(name="stat", bufs=3))
         out_pool = ctx.enter_context(tc.tile_pool(name="out", bufs=6))
-        hid_pool = ctx.enter_context(tc.tile_pool(name="hid", bufs=B))
+        hid_pool = ctx.enter_context(tc.tile_pool(name="hid", bufs=2))
         xt_psum = ctx.enter_context(tc.psum_pool(name="xt", bufs=4))
         acc_psum = ctx.enter_context(tc.psum_pool(name="acc", bufs=4))
         ctx.enter_context(tc.manual_schedule())
@@ -98,6 +98,7 @@ def tile_dflashattention_pa_t_kernel(
                 )
 
         norm_w = const.tile([P, 2, D], BF16, name="norm_w")
+        norm_w_sin = const.tile([P, 2, D], BF16, name="norm_w_sin")
         cos_ctx = const.tile([P, B * J, D], BF16, name="cos_ctx")
         sin_ctx = const.tile([P, B * J, D], BF16, name="sin_ctx")
         cos_new = const.tile([P, B, D], BF16, name="cos_new")
@@ -125,6 +126,9 @@ def tile_dflashattention_pa_t_kernel(
                 stop=True,
             )
             nc.vector.tensor_copy(out=norm_w[:].rearrange("p a d -> p (a d)"), in_=spread[:, 0 : 2 * D])
+            rows = spread[:, 0 : 2 * D].rearrange("p (a d) -> p a d", a=2)
+            nc.vector.tensor_copy(out=norm_w_sin[:, :, 0:HALF], in_=rows[:, :, 0:HALF])
+            nc.vector.tensor_scalar_mul(out=norm_w_sin[:, :, HALF:D], in0=rows[:, :, HALF:D], scalar1=-1.0)
 
         def load_ctx_tables(b, queue):
             for table, dst in ((cos, cos_ctx), (sin, sin_ctx)):
@@ -200,6 +204,7 @@ def tile_dflashattention_pa_t_kernel(
                 c = cos_new[:, i : i + 2, :].unsqueeze(2).to_broadcast(shape)
                 sn = sin_new[:, i : i + 2, :].unsqueeze(2).to_broadcast(shape)
                 w = norm_w[:].unsqueeze(1).to_broadcast(shape)
+                ws = norm_w_sin[:].unsqueeze(1).to_broadcast(shape)
             else:
                 c = cos_ctx[:, 2 * i : 2 * i + 4, :].rearrange("p (s t) d -> p s t d", s=2)
                 sn = sin_ctx[:, 2 * i : 2 * i + 4, :].rearrange("p (s t) d -> p s t d", s=2)
@@ -208,16 +213,16 @@ def tile_dflashattention_pa_t_kernel(
             nc.gpsimd.tensor_tensor(out=tab[:, :, :, 0, :], in0=c, in1=w, op=ALU.mult)
             if kind == "new":
                 nc.gpsimd.tensor_tensor(
-                    out=tab[:, :, :, 1, 0:HALF], in0=sn[:, :, :, HALF:D], in1=w[:, :, :, 0:HALF], op=ALU.mult
+                    out=tab[:, :, :, 1, 0:HALF], in0=sn[:, :, :, HALF:D], in1=ws[:, :, :, 0:HALF], op=ALU.mult
                 )
                 nc.gpsimd.tensor_tensor(
-                    out=tab[:, :, :, 1, HALF:D], in0=sn[:, :, :, 0:HALF], in1=w[:, :, :, HALF:D], op=ALU.mult
+                    out=tab[:, :, :, 1, HALF:D], in0=sn[:, :, :, 0:HALF], in1=ws[:, :, :, HALF:D], op=ALU.mult
                 )
             else:
                 nc.gpsimd.tensor_tensor(
                     out=tab[:].rearrange("p s t c (a e) -> p (s t) c a e", a=2)[:, :, 1, :, :],
                     in0=sin_ctx[:, 2 * i : 2 * i + 4, :].rearrange("p n (a e) -> p n a e", a=2)[:, :, ::-1, :],
-                    in1=norm_w[:, 0:1, :].to_broadcast([P, 4, D]).rearrange("p n (a e) -> p n a e", a=2),
+                    in1=norm_w_sin[:, 0:1, :].to_broadcast([P, 4, D]).rearrange("p n (a e) -> p n a e", a=2),
                     op=ALU.mult,
                 )
             tables[s] = tab[:, 0]
@@ -253,27 +258,48 @@ def tile_dflashattention_pa_t_kernel(
             )
             x_codes[s] = (codes, plane)
 
-        def banks_of(s):
-            if steps[s][0] == "new":
-                return [(0, w_kv, s_kv, KVH, 0), (0, w_q, s_q, H, KVH)]
-            return [(0, w_kv, s_kv, KVH, 0), (1, w_kv, s_kv, KVH, KVH)]
-
-        def project(s, bank):
+        def project_step(s):
             codes, plane = x_codes[s]
-            t, w_tile, s_tile, heads, slot = banks_of(s)[bank]
-            acc = acc_psum.tile([P, N_BANK], F32, name="acc", tag="acc")
-            for g in range(PASSES):
-                cols = slice((t * PASSES + g) * P, (t * PASSES + g + 1) * P)
-                nc.tensor.matmul_mx(
-                    out=acc[:],
-                    lhsT=codes[:, cols].bitcast(FP8X4),
-                    lhsT_scale=plane[:, cols],
-                    rhs=w_tile[:, g, :].bitcast(FP4X4),
-                    rhs_scale=s_tile[:, g, :],
-                    start=(g == 0),
-                    stop=(g == PASSES - 1),
-                )
-            acc_banks.setdefault(s, []).append(acc)
+            banks = []
+            if steps[s][0] == "new":
+                for w_tile, s_tile in ((w_kv, s_kv), (w_q, s_q)):
+                    acc = acc_psum.tile([P, N_BANK], F32, name="acc", tag="acc")
+                    for g in range(PASSES):
+                        cols = slice(g * P, (g + 1) * P)
+                        nc.tensor.matmul_mx(
+                            out=acc[:],
+                            lhsT=codes[:, cols].bitcast(FP8X4),
+                            lhsT_scale=plane[:, cols],
+                            rhs=w_tile[:, g, :].bitcast(FP4X4),
+                            rhs_scale=s_tile[:, g, :],
+                            start=(g == 0),
+                            stop=(g == PASSES - 1),
+                        )
+                    banks.append(acc)
+            else:
+                for part in range(2):
+                    acc = acc_psum.tile([P, N_BANK], F32, name="acc", tag="acc")
+                    for t in range(2):
+                        for h in range(KVH):
+                            col = (part * KVH + h) * D
+                            for g in range(PASSES):
+                                cols = slice((t * PASSES + g) * P, (t * PASSES + g + 1) * P)
+                                nc.tensor.matmul_mx(
+                                    out=acc[:, (t * KVH + h) * D : (t * KVH + h + 1) * D],
+                                    lhsT=codes[:, cols].bitcast(FP8X4),
+                                    lhsT_scale=plane[:, cols],
+                                    rhs=w_kv[:, g, 2 * col : 2 * (col + D)].bitcast(FP4X4),
+                                    rhs_scale=s_kv[:, g, col : col + D],
+                                    start=(g == 0),
+                                    stop=(g == PASSES - 1),
+                                )
+                    banks.append(acc)
+            acc_banks[s] = banks
+
+        def heads_of(s):
+            if steps[s][0] == "new":
+                return [(0, h, 0) for h in range(KVH)] + [(1, h, 1) for h in range(H)]
+            return [(0, t * KVH + h, t) for t in range(2) for h in range(KVH)]
 
         def out_tile_of(s):
             kind, i = steps[s]
@@ -288,18 +314,17 @@ def tile_dflashattention_pa_t_kernel(
         def sum_squares(s):
             squares = rope_pool.tile([P, KVH + H, D], BF16, name="squares", tag="squares")
             sums = stat_pool.tile([P, KVH + H], F32, name="sums", tag="sums")
-            for acc, (t, w_tile, s_tile, heads, slot) in zip(acc_banks[s], banks_of(s)):
-                for h in range(heads):
-                    nc.scalar.activation(
-                        out=squares[:, slot + h, :],
-                        in_=acc[:, h * D : (h + 1) * D],
-                        func=ACT.Square,
-                        accum_out=sums[:, slot + h : slot + h + 1],
-                    )
+            for n, (bank, place, table) in enumerate(heads_of(s)):
+                nc.scalar.activation(
+                    out=squares[:, n, :],
+                    in_=acc_banks[s][bank][:, place * D : (place + 1) * D],
+                    func=ACT.Square,
+                    accum_out=sums[:, n : n + 1],
+                )
             return sums
 
         def inverse_rms(s, sums):
-            n_heads = sum(heads for t, w_tile, s_tile, heads, slot in banks_of(s))
+            n_heads = len(heads_of(s))
             inv = stat_pool.tile([P, KVH + H], F32, name="inv", tag="inv")
             nc.scalar.activation(
                 out=inv[:, 0:n_heads],
@@ -314,41 +339,58 @@ def tile_dflashattention_pa_t_kernel(
             kind, i = steps[s]
             o = out_tile_of(s)
             if kind == "new":
-                v_dst = [o[:, KVH + H :, :]]
+                nc.scalar.copy(
+                    out=o[:, KVH + H :, :],
+                    in_=acc_banks[s][0][:, KVH * D : 2 * KVH * D].rearrange("p (h d) -> p h d", h=KVH),
+                )
             else:
-                v_dst = [o[:, 1, :, (2 * i + t) % CHUNK, :] for t in range(2)]
-            for acc, dst in zip(acc_banks[s], v_dst):
-                nc.scalar.copy(out=dst, in_=acc[:, KVH * D : 2 * KVH * D].rearrange("p (h d) -> p h d", h=KVH))
+                first = 2 * i % CHUNK
+                nc.scalar.copy(
+                    out=o[:, 1, :, first : first + 2, :].rearrange("p h t d -> p t h d"),
+                    in_=acc_banks[s][1][:].rearrange("p (t h d) -> p t h d", t=2, h=KVH),
+                )
 
         def rotate(s, inv):
-            prod = rope_pool.tile([P, KVH + H, 2, D], F32, name="prod", tag="prod")
-            for bank, (acc, (t, w_tile, s_tile, heads, slot)) in enumerate(zip(acc_banks[s], banks_of(s))):
-                for h in range(heads):
-                    nc.vector.scalar_tensor_tensor(
-                        out=prod[:, slot + h, :, :],
-                        in0=acc[:, h * D : (h + 1) * D].unsqueeze(1).to_broadcast([P, 2, D]),
-                        scalar=inv[:, slot + h : slot + h + 1],
-                        in1=tables[s][:, bank, :, :],
-                        op0=ALU.mult,
-                        op1=ALU.mult,
-                    )
-            products[s] = prod
+            kind, i = steps[s]
+            if kind == "new":
+                prod = rope_pool.tile([P, KVH * CHUNK, 2, D], F32, name="prod", tag="prod")
+                products[s] = prod
+                places = list(range(KVH + H))
+            else:
+                first = 2 * i % CHUNK
+                if first == 0:
+                    prod = rope_pool.tile([P, KVH * CHUNK, 2, D], F32, name="prod", tag="prod")
+                    products[s] = prod
+                    products[s + 1] = prod
+                prod = products[s]
+                places = [h * CHUNK + first + t for t in range(2) for h in range(KVH)]
+            for n, (bank, place, table) in enumerate(heads_of(s)):
+                nc.vector.scalar_tensor_tensor(
+                    out=prod[:, places[n], :, :],
+                    in0=acc_banks[s][bank][:, place * D : (place + 1) * D].unsqueeze(1).to_broadcast([P, 2, D]),
+                    scalar=inv[:, n : n + 1],
+                    in1=tables[s][:, table, :, :],
+                    op0=ALU.mult,
+                    op1=ALU.mult,
+                )
 
         def add_halves(s):
             kind, i = steps[s]
             o = out_tile_of(s)
             if kind == "new":
-                dst = o[:, 0 : KVH + H, :].unsqueeze(1)
-                src = products[s][:].unsqueeze(1)
+                n_heads = KVH + H
+                dst = o[:, 0:n_heads, :]
+            elif (2 * i + 2) % CHUNK == 0:
+                n_heads = KVH * CHUNK
+                dst = o[:, 0].rearrange("p h t d -> p (h t) d")
             else:
-                first = 2 * i % CHUNK
-                dst = o[:, 0, :, first : first + 2, :]
-                src = products[s][:, 0 : 2 * KVH].rearrange("p (t h) c d -> p h t c d", t=2)
+                return
+            src = products[s][:, 0:n_heads].rearrange("p n c (a e) -> p n c a e", a=2)
             nc.vector.tensor_tensor(
-                out=dst[:, :, :, 0:HALF], in0=src[:, :, :, 0, 0:HALF], in1=src[:, :, :, 1, HALF:D], op=ALU.subtract
-            )
-            nc.vector.tensor_tensor(
-                out=dst[:, :, :, HALF:D], in0=src[:, :, :, 0, HALF:D], in1=src[:, :, :, 1, 0:HALF], op=ALU.add
+                out=dst.rearrange("p n (a e) -> p n a e", a=2),
+                in0=src[:, :, 0, :, :],
+                in1=src[:, :, 1, ::-1, :],
+                op=ALU.add,
             )
 
         def store(s, which):
@@ -402,10 +444,6 @@ def tile_dflashattention_pa_t_kernel(
             regroup_x(s)
             quantise_x(s)
 
-        def project_step(s):
-            project(s, 0)
-            project(s, 1)
-
         warm_up()
         transposes(0)
         spread_norm_weights()
@@ -436,14 +474,12 @@ def tile_dflashattention_pa_t_kernel(
                 after_projection(first - 3)
             if live(first - 1):
                 project_step(first - 1)
-            if live(first - 4):
-                add_halves(first - 4)
-                store(first - 4, 0)
             if live(first):
                 prepare(first)
-            if live(first - 3):
-                add_halves(first - 3)
-                store(first - 3, 0)
+            for s in (first - 4, first - 3):
+                if live(s):
+                    add_halves(s)
+                    store(s, 0)
             if live(first + 1):
                 prepare(first + 1)
             if live(first - 2):

@@ -28,7 +28,7 @@ J = CTX // P
 CHUNK = 4
 LOAD_AHEAD = 26
 WARM_UP = 4
-NEW_AFTER = 8
+NEW_AFTER = (4, 16)
 
 FLOPS = 2 * HID * (B * Q_LEN * H * D + 2 * B * T * KVH * D)
 
@@ -145,8 +145,8 @@ def tile_dflashattention_pa_t_kernel(
         steps = []
         for m in range(pairs):
             steps.append(("ctx", m))
-            if (m + 1) % NEW_AFTER == 0:
-                b = 2 * ((m + 1) // NEW_AFTER - 1)
+            if m + 1 in NEW_AFTER:
+                b = 2 * NEW_AFTER.index(m + 1)
                 steps.append(("new", b))
                 steps.append(("new", b + 1))
         assert len(steps) == pairs + B
@@ -380,6 +380,19 @@ def tile_dflashattention_pa_t_kernel(
             if kind == "new":
                 n_heads = KVH + H
                 dst = o[:, 0:n_heads, :]
+            elif s >= n_steps - 2:
+                first = 2 * i % CHUNK
+                for h in range(KVH):
+                    src = products[s][:, h * CHUNK + first : h * CHUNK + first + 2].rearrange(
+                        "p n c (a e) -> p n c a e", a=2
+                    )
+                    nc.vector.tensor_tensor(
+                        out=o[:, 0, h, first : first + 2, :].rearrange("p n (a e) -> p n a e", a=2),
+                        in0=src[:, :, 0, :, :],
+                        in1=src[:, :, 1, ::-1, :],
+                        op=ALU.add,
+                    )
+                return
             elif (2 * i + 2) % CHUNK == 0:
                 n_heads = KVH * CHUNK
                 dst = o[:, 0].rearrange("p h t d -> p (h t) d")
@@ -402,16 +415,17 @@ def tile_dflashattention_pa_t_kernel(
                 nc.sync.dma_start(out=out[i, :, CTX:T, :].rearrange("h t d -> t h d"), in_=heads)
                 if which == 0:
                     nc.sync.dma_start(out=out_q[i].rearrange("h t d -> t h d"), in_=o[:, KVH : KVH + H, :])
-            elif (2 * i + 2) % CHUNK == 0:
+            elif (2 * i + 2) % CHUNK == 0 or s >= n_steps - 2:
                 n_last = 2 * i + 2
-                n_first = n_last - CHUNK
+                n_first = n_last - (2 if s >= n_steps - 2 else CHUNK)
+                base = 2 * i // CHUNK * CHUNK
                 for b in range(B):
                     lo, hi = max(n_first, b * J), min(n_last, (b + 1) * J)
                     if lo < hi:
                         rows = out[b, :, 0:CTX, :].rearrange("h (p j) d -> p h j d", j=J)
                         nc.sync.dma_start(
                             out=rows[:, :, lo - b * J : hi - b * J, :],
-                            in_=o[:, which, :, lo - n_first : hi - n_first, :],
+                            in_=o[:, which, :, lo - base : hi - base, :],
                         )
 
         load_ctx_tables(0, nc.gpsimd)
@@ -431,9 +445,14 @@ def tile_dflashattention_pa_t_kernel(
 
         def after_projection(s):
             sums = sum_squares(s)
-            copy_v(s)
-            store(s, 1)
-            inv = inverse_rms(s, sums)
+            if s == n_steps - 1:
+                inv = inverse_rms(s, sums)
+                copy_v(s)
+                store(s, 1)
+            else:
+                copy_v(s)
+                store(s, 1)
+                inv = inverse_rms(s, sums)
             rotate(s, inv)
 
         def transposes(s):
@@ -470,6 +489,10 @@ def tile_dflashattention_pa_t_kernel(
                 make_tables(first)
             if live(first - 2):
                 project_step(first - 2)
+            early = first - 4 == n_steps - 2
+            if early:
+                add_halves(first - 4)
+                store(first - 4, 0)
             if live(first - 3) and r > 2:
                 after_projection(first - 3)
             if live(first - 1):
@@ -477,7 +500,7 @@ def tile_dflashattention_pa_t_kernel(
             if live(first):
                 prepare(first)
             for s in (first - 4, first - 3):
-                if live(s):
+                if live(s) and not (early and s == first - 4):
                     add_halves(s)
                     store(s, 0)
             if live(first + 1):

@@ -187,9 +187,7 @@ def tile_dflashattention_pa_t_kernel(
                 b1, j1 = divmod(2 * i + 1, J)
                 if s == 0:
                     for t in range(2):
-                        for g in range(PASSES):
-                            k_cols = slice(g * K_PASS, (g + 1) * K_PASS)
-                            nc.sync.dma_start(out=x_sb[:, t, k_cols], in_=ctx_x[b0, :, j0 + t, k_cols])
+                        nc.sync.dma_start(out=x_sb[:, t, :], in_=ctx_x[b0, :, j0 + t, :])
                 elif b0 == b1:
                     nc.sync.dma_start(out=x_sb[:], in_=ctx_x[b0, :, j0 : j0 + 2, :])
                 else:

from contextlib import ExitStack

import concourse.masks as masks
import concourse.mybir as mybir

F32 = mybir.dt.float32
BF16 = mybir.dt.bfloat16
I32 = mybir.dt.int32
U32 = mybir.dt.uint32
U8 = mybir.dt.uint8
FP8X4 = mybir.dt.float8_e4m3fn_x4
FP4X4 = mybir.dt.float4_e2m1fn_x4
ACT = mybir.ActivationFunctionType
ALU = mybir.AluOpType

B, Q_LEN, CTX, HID, H, KVH, D = 4, 128, 1408, 1024, 4, 2, 128
T = CTX + Q_LEN
EPS = 1e-6
HALF = D // 2

P = 128
PACK = 4
K_PASS = P * PACK
PASSES = HID // K_PASS
WORDS = HID // 2
N_BANK = 512
J = CTX // P
CHUNK = 4
LOAD_AHEAD = 26
WARM_UP = 4
NEW_AFTER = (4, 16)

FLOPS = 2 * HID * (B * Q_LEN * H * D + 2 * B * T * KVH * D)


def tile_dflashattention_pa_t_kernel(
    tc,
    hidden_states,
    target_hidden,
    cos,
    sin,
    Wq_words,
    Wq_scales,
    Wk_words,
    Wk_scales,
    Wv_words,
    Wv_scales,
    q_norm_w,
    k_norm_w,
    out_q,
    out_k,
    out_v,
):
    nc = tc.nc
    with ExitStack() as ctx:
        const = ctx.enter_context(tc.tile_pool(name="const", bufs=1))
        x_pool = ctx.enter_context(tc.tile_pool(name="x", bufs=1))
        tab_pool = ctx.enter_context(tc.tile_pool(name="tab", bufs=3))
        mx_pool = ctx.enter_context(tc.tile_pool(name="mx", bufs=2))
        code_pool = ctx.enter_context(tc.tile_pool(name="code", bufs=4))
        rope_pool = ctx.enter_context(tc.tile_pool(name="rope", bufs=2))
        stat_pool = ctx.enter_context(tc.tile_pool(name="stat", bufs=3))
        out_pool = ctx.enter_context(tc.tile_pool(name="out", bufs=6))
        hid_pool = ctx.enter_context(tc.tile_pool(name="hid", bufs=2))
        xt_psum = ctx.enter_context(tc.psum_pool(name="xt", bufs=4))
        acc_psum = ctx.enter_context(tc.psum_pool(name="acc", bufs=4))
        ctx.enter_context(tc.manual_schedule())

        ones = const.tile([P, P], BF16, name="ones")
        nc.vector.memset(ones[:], 1.0)
        zeros = const.tile([P, N_BANK], BF16, name="zeros")
        nc.vector.memset(zeros[:], 0.0)
        ident = const.tile([P, P], F32, name="ident")
        masks.make_identity(nc, ident[:])
        eps = const.tile([P, 1], F32, name="eps")
        nc.vector.memset(eps[:], EPS)
        warm = const.tile([P, 1], F32, name="warm")
        nc.scalar.activation(out=warm[:], in_=eps[:], func=ACT.Abs_reciprocal_sqrt)

        w_kv = const.tile([P, PASSES, 2 * N_BANK], U8, name="w_kv", align_bytes=64)
        s_kv = const.tile([P, PASSES, N_BANK], U8, name="s_kv", align_bytes=64)
        w_q = const.tile([P, PASSES, 2 * N_BANK], U8, name="w_q", align_bytes=64)
        s_q = const.tile([P, PASSES, N_BANK], U8, name="s_q", align_bytes=64)
        nc.vector.memset(s_kv[:].bitcast(I32), 0)
        nc.vector.memset(s_q[:].bitcast(I32), 0)

        def load_words(words, w_tile, col0, cols):
            nc.sync.dma_start(
                out=w_tile[:, :, 2 * col0 : 2 * (col0 + cols)].bitcast(I32),
                in_=words.bitcast(I32).rearrange("g p n -> p g n"),
            )

        def load_scales(scales, s_tile, col0, cols):
            for quad in range(4):
                nc.sync.dma_start(
                    out=s_tile[32 * quad : 32 * quad + 4, :, col0 : col0 + cols].bitcast(I32),
                    in_=scales.bitcast(I32)[:, 4 * quad : 4 * quad + 4, :].rearrange("g r n -> r g n"),
                )

        norm_w = const.tile([P, 2, D], BF16, name="norm_w")
        norm_w_sin = const.tile([P, 2, D], BF16, name="norm_w_sin")
        cos_ctx = const.tile([P, B * J, D], BF16, name="cos_ctx")
        sin_ctx = const.tile([P, B * J, D], BF16, name="sin_ctx")
        cos_new = const.tile([P, B, D], BF16, name="cos_new")
        sin_new = const.tile([P, B, D], BF16, name="sin_new")

        w_rows = const.tile([P, 2, D], BF16, name="w_rows")
        nc.vector.memset(w_rows[:], 0.0)

        def warm_up():
            idle = acc_psum.tile([P, N_BANK], F32, name="acc", tag="acc")
            for n in range(WARM_UP):
                nc.tensor.matmul(out=idle[:], lhsT=ones[:], rhs=zeros[:], start=True, stop=True)

        def load_norm_rows():
            nc.sync.dma_start(out=w_rows[0:1, 0, :], in_=k_norm_w.unsqueeze(0))
            nc.sync.dma_start(out=w_rows[0:1, 1, :], in_=q_norm_w.unsqueeze(0))

        def spread_norm_weights():
            spread = acc_psum.tile([P, N_BANK], F32, name="acc", tag="acc")
            nc.tensor.matmul(
                out=spread[:, 0 : 2 * D],
                lhsT=ones[:],
                rhs=w_rows[:].rearrange("p a d -> p (a d)"),
                start=True,
                stop=True,
            )
            nc.vector.tensor_copy(out=norm_w[:].rearrange("p a d -> p (a d)"), in_=spread[:, 0 : 2 * D])
            rows = spread[:, 0 : 2 * D].rearrange("p (a d) -> p a d", a=2)
            nc.vector.tensor_copy(out=norm_w_sin[:, :, 0:HALF], in_=rows[:, :, 0:HALF])
            nc.vector.tensor_scalar_mul(out=norm_w_sin[:, :, HALF:D], in0=rows[:, :, HALF:D], scalar1=-1.0)

        def load_ctx_tables(b, queue):
            for table, dst in ((cos, cos_ctx), (sin, sin_ctx)):
                queue.dma_start(
                    out=dst[:, b * J : (b + 1) * J, :],
                    in_=table[b, 0:CTX, :].rearrange("(p j) d -> p j d", j=J),
                )

        def load_new_tables():
            for table, dst in ((cos, cos_new), (sin, sin_new)):
                nc.sync.dma_start(out=dst[:], in_=table[:, CTX:T, :].rearrange("b t d -> t b d"))

        pairs = B * J // 2
        steps = []
        for m in range(pairs):
            steps.append(("ctx", m))
            if m + 1 in NEW_AFTER:
                b = 2 * NEW_AFTER.index(m + 1)
                steps.append(("new", b))
                steps.append(("new", b + 1))
        assert len(steps) == pairs + B
        n_steps = len(steps)
        ctx_x = target_hidden.rearrange("b (p j) k -> b p j k", j=J)

        x_tiles = {}
        xt_banks = {}
        grouped = {}
        x_codes = {}
        acc_banks = {}
        tables = {}
        products = {}
        out_tiles = {}

        def load_tables_for(s):
            kind, i = steps[s]
            if kind == "new":
                if i == 0:
                    load_new_tables()
            else:
                for n in (2 * i, 2 * i + 1):
                    if n % J == 0:
                        load_ctx_tables(n // J, nc.sync)

        def load_x(s):
            kind, i = steps[s]
            if kind == "new":
                if i == 0:
                    load_words(Wq_words, w_q, 0, H * D)
                    load_scales(Wq_scales, s_q, 0, H * D)
                x_sb = x_pool.tile([P, 1, HID], BF16, name="x_new%d" % i)
                nc.sync.dma_start(out=x_sb[:, 0, :], in_=hidden_states[i])
                x_tiles[s] = [x_sb[:, 0, :].bitcast(F32)]
            else:
                x_sb = x_pool.tile([P, 2, HID], BF16, name="x_ctx%d" % i)
                b0, j0 = divmod(2 * i, J)
                b1, j1 = divmod(2 * i + 1, J)
                if s == 0:
                    for t in range(2):
                        nc.sync.dma_start(out=x_sb[:, t, :], in_=ctx_x[b0, :, j0 + t, :])
                elif b0 == b1:
                    nc.sync.dma_start(out=x_sb[:], in_=ctx_x[b0, :, j0 : j0 + 2, :])
                else:
                    nc.sync.dma_start(out=x_sb[:, 0, :], in_=ctx_x[b0, :, j0, :])
                    nc.sync.dma_start(out=x_sb[:, 1, :], in_=ctx_x[b1, :, j1, :])
                x_tiles[s] = [x_sb[:, 0, :].bitcast(F32), x_sb[:, 1, :].bitcast(F32)]

        def make_tables(s):
            kind, i = steps[s]
            shape = [P, 2, 2, D]
            if kind == "new":
                c = cos_new[:, i : i + 2, :].unsqueeze(2).to_broadcast(shape)
                sn = sin_new[:, i : i + 2, :].unsqueeze(2).to_broadcast(shape)
                w = norm_w[:].unsqueeze(1).to_broadcast(shape)
                ws = norm_w_sin[:].unsqueeze(1).to_broadcast(shape)
            else:
                c = cos_ctx[:, 2 * i : 2 * i + 4, :].rearrange("p (s t) d -> p s t d", s=2)
                sn = sin_ctx[:, 2 * i : 2 * i + 4, :].rearrange("p (s t) d -> p s t d", s=2)
                w = norm_w[:, 0:1, :].unsqueeze(1).to_broadcast(shape)
            tab = tab_pool.tile([P, 2, 2, 2, D], F32, name="tab", tag="tab")
            nc.gpsimd.tensor_tensor(out=tab[:, :, :, 0, :], in0=c, in1=w, op=ALU.mult)
            if kind == "new":
                nc.gpsimd.tensor_tensor(
                    out=tab[:, :, :, 1, 0:HALF], in0=sn[:, :, :, HALF:D], in1=ws[:, :, :, 0:HALF], op=ALU.mult
                )
                nc.gpsimd.tensor_tensor(
                    out=tab[:, :, :, 1, HALF:D], in0=sn[:, :, :, 0:HALF], in1=ws[:, :, :, HALF:D], op=ALU.mult
                )
            else:
                nc.gpsimd.tensor_tensor(
                    out=tab[:].rearrange("p s t c (a e) -> p (s t) c a e", a=2)[:, :, 1, :, :],
                    in0=sin_ctx[:, 2 * i : 2 * i + 4, :].rearrange("p n (a e) -> p n a e", a=2)[:, :, ::-1, :],
                    in1=norm_w_sin[:, 0:1, :].to_broadcast([P, 4, D]).rearrange("p n (a e) -> p n a e", a=2),
                    op=ALU.mult,
                )
            tables[s] = tab[:, 0]
            tables[s + 1] = tab[:, 1]

        def transpose_x(s, t):
            words = x_tiles[s][t]
            xt = xt_psum.tile([P, PASSES, 2, P], F32, name="xt", tag="xt")
            for g in range(PASSES):
                for u in range(2):
                    nc.tensor.transpose(
                        out=xt[:, g, u, :],
                        in_=words[:, g * (WORDS // PASSES) + u : (g + 1) * (WORDS // PASSES) : 2],
                        identity=ident[:],
                    )
            xt_banks.setdefault(s, []).append(xt)

        def regroup_x(s):
            grp = mx_pool.tile([P, 2 * PASSES * P * PACK], BF16, name="grp", tag="grp", align_bytes=64)
            grp_words = grp[:].bitcast(F32).rearrange("p (t g r u) -> p t g r u", t=2, g=PASSES, u=2)
            for t, xt in enumerate(xt_banks[s]):
                nc.scalar.copy(out=grp_words[:, t], in_=xt[:].rearrange("p g u r -> p g r u"))
            grouped[s] = grp

        def quantise_x(s):
            cols = len(x_tiles[s]) * PASSES * P
            codes = code_pool.tile([P, 2 * PASSES * P], U32, name="codes", tag="codes", align_bytes=64)
            plane = code_pool.tile([P, 2 * PASSES * P], U8, name="plane", tag="plane", align_bytes=64)
            nc.vector.quantize_mx(
                out=codes[:, 0:cols].bitcast(FP8X4),
                scales=plane[:, 0:cols],
                in_=grouped[s][:, 0 : cols * PACK],
            )
            x_codes[s] = (codes, plane)

        def project_step(s):
            codes, plane = x_codes[s]
            banks = []
            if steps[s][0] == "new":
                for w_tile, s_tile in ((w_kv, s_kv), (w_q, s_q)):
                    acc = acc_psum.tile([P, N_BANK], F32, name="acc", tag="acc")
                    for g in range(PASSES):
                        cols = slice(g * P, (g + 1) * P)
                        nc.tensor.matmul_mx(
                            out=acc[:],
                            lhsT=codes[:, cols].bitcast(FP8X4),
                            lhsT_scale=plane[:, cols],
                            rhs=w_tile[:, g, :].bitcast(FP4X4),
                            rhs_scale=s_tile[:, g, :],
                            start=(g == 0),
                            stop=(g == PASSES - 1),
                        )
                    banks.append(acc)
            else:
                for part in range(2):
                    acc = acc_psum.tile([P, N_BANK], F32, name="acc", tag="acc")
                    for t in range(2):
                        for h in range(KVH):
                            col = (part * KVH + h) * D
                            for g in range(PASSES):
                                cols = slice((t * PASSES + g) * P, (t * PASSES + g + 1) * P)
                                nc.tensor.matmul_mx(
                                    out=acc[:, (t * KVH + h) * D : (t * KVH + h + 1) * D],
                                    lhsT=codes[:, cols].bitcast(FP8X4),
                                    lhsT_scale=plane[:, cols],
                                    rhs=w_kv[:, g, 2 * col : 2 * (col + D)].bitcast(FP4X4),
                                    rhs_scale=s_kv[:, g, col : col + D],
                                    start=(g == 0),
                                    stop=(g == PASSES - 1),
                                )
                    banks.append(acc)
            acc_banks[s] = banks

        def heads_of(s):
            if steps[s][0] == "new":
                return [(0, h, 0) for h in range(KVH)] + [(1, h, 1) for h in range(H)]
            return [(0, t * KVH + h, t) for t in range(2) for h in range(KVH)]

        def out_tile_of(s):
            kind, i = steps[s]
            key = s if kind == "new" else ("ctx", 2 * i // CHUNK)
            if key not in out_tiles:
                if kind == "new":
                    out_tiles[key] = hid_pool.tile([P, KVH + H + KVH, D], F32, name="o_new", tag="o_new")
                else:
                    out_tiles[key] = out_pool.tile([P, 2, KVH, CHUNK, D], F32, name="o_ctx", tag="o_ctx")
            return out_tiles[key]

        def sum_squares(s):
            squares = rope_pool.tile([P, KVH + H, D], BF16, name="squares", tag="squares")
            sums = stat_pool.tile([P, KVH + H], F32, name="sums", tag="sums")
            for n, (bank, place, table) in enumerate(heads_of(s)):
                nc.scalar.activation(
                    out=squares[:, n, :],
                    in_=acc_banks[s][bank][:, place * D : (place + 1) * D],
                    func=ACT.Square,
                    accum_out=sums[:, n : n + 1],
                )
            return sums

        def inverse_rms(s, sums):
            n_heads = len(heads_of(s))
            inv = stat_pool.tile([P, KVH + H], F32, name="inv", tag="inv")
            nc.scalar.activation(
                out=inv[:, 0:n_heads],
                in_=sums[:, 0:n_heads],
                func=ACT.Abs_reciprocal_sqrt,
                bias=eps[:],
                scale=1.0 / D,
            )
            return inv

        def copy_v(s):
            kind, i = steps[s]
            o = out_tile_of(s)
            if kind == "new":
                nc.scalar.copy(
                    out=o[:, KVH + H :, :],
                    in_=acc_banks[s][0][:, KVH * D : 2 * KVH * D].rearrange("p (h d) -> p h d", h=KVH),
                )
            else:
                first = 2 * i % CHUNK
                nc.scalar.copy(
                    out=o[:, 1, :, first : first + 2, :].rearrange("p h t d -> p t h d"),
                    in_=acc_banks[s][1][:].rearrange("p (t h d) -> p t h d", t=2, h=KVH),
                )

        def rotate(s, inv):
            kind, i = steps[s]
            if kind == "new":
                prod = rope_pool.tile([P, KVH * CHUNK, 2, D], F32, name="prod", tag="prod")
                products[s] = prod
                places = list(range(KVH + H))
            else:
                first = 2 * i % CHUNK
                if first == 0:
                    prod = rope_pool.tile([P, KVH * CHUNK, 2, D], F32, name="prod", tag="prod")
                    products[s] = prod
                    products[s + 1] = prod
                prod = products[s]
                places = [h * CHUNK + first + t for t in range(2) for h in range(KVH)]
            for n, (bank, place, table) in enumerate(heads_of(s)):
                nc.vector.scalar_tensor_tensor(
                    out=prod[:, places[n], :, :],
                    in0=acc_banks[s][bank][:, place * D : (place + 1) * D].unsqueeze(1).to_broadcast([P, 2, D]),
                    scalar=inv[:, n : n + 1],
                    in1=tables[s][:, table, :, :],
                    op0=ALU.mult,
                    op1=ALU.mult,
                )

        def add_halves(s):
            kind, i = steps[s]
            o = out_tile_of(s)
            if kind == "new":
                n_heads = KVH + H
                dst = o[:, 0:n_heads, :]
            elif s >= n_steps - 2:
                first = 2 * i % CHUNK
                for h in range(KVH):
                    src = products[s][:, h * CHUNK + first : h * CHUNK + first + 2].rearrange(
                        "p n c (a e) -> p n c a e", a=2
                    )
                    nc.vector.tensor_tensor(
                        out=o[:, 0, h, first : first + 2, :].rearrange("p n (a e) -> p n a e", a=2),
                        in0=src[:, :, 0, :, :],
                        in1=src[:, :, 1, ::-1, :],
                        op=ALU.add,
                    )
                return
            elif (2 * i + 2) % CHUNK == 0:
                n_heads = KVH * CHUNK
                dst = o[:, 0].rearrange("p h t d -> p (h t) d")
            else:
                return
            src = products[s][:, 0:n_heads].rearrange("p n c (a e) -> p n c a e", a=2)
            nc.vector.tensor_tensor(
                out=dst.rearrange("p n (a e) -> p n a e", a=2),
                in0=src[:, :, 0, :, :],
                in1=src[:, :, 1, ::-1, :],
                op=ALU.add,
            )

        def store(s, which):
            kind, i = steps[s]
            o = out_tile_of(s)
            out = (out_k, out_v)[which]
            if kind == "new":
                heads = (o[:, 0:KVH, :], o[:, KVH + H :, :])[which]
                nc.sync.dma_start(out=out[i, :, CTX:T, :].rearrange("h t d -> t h d"), in_=heads)
                if which == 0:
                    nc.sync.dma_start(out=out_q[i].rearrange("h t d -> t h d"), in_=o[:, KVH : KVH + H, :])
            elif (2 * i + 2) % CHUNK == 0 or s >= n_steps - 2:
                n_last = 2 * i + 2
                n_first = n_last - (2 if s >= n_steps - 2 else CHUNK)
                base = 2 * i // CHUNK * CHUNK
                for b in range(B):
                    lo, hi = max(n_first, b * J), min(n_last, (b + 1) * J)
                    if lo < hi:
                        rows = out[b, :, 0:CTX, :].rearrange("h (p j) d -> p h j d", j=J)
                        nc.sync.dma_start(
                            out=rows[:, :, lo - b * J : hi - b * J, :],
                            in_=o[:, which, :, lo - base : hi - base, :],
                        )

        load_ctx_tables(0, nc.gpsimd)
        load_x(0)
        load_x(1)
        load_norm_rows()
        load_words(Wk_words, w_kv, 0, KVH * D)
        load_words(Wv_words, w_kv, KVH * D, KVH * D)
        load_scales(Wk_scales, s_kv, 0, KVH * D)
        load_scales(Wv_scales, s_kv, KVH * D, KVH * D)
        for s in range(2, LOAD_AHEAD):
            load_x(s)
            load_tables_for(s)

        def live(s):
            return 0 <= s < n_steps

        def after_projection(s):
            sums = sum_squares(s)
            if s == n_steps - 1:
                inv = inverse_rms(s, sums)
                copy_v(s)
                store(s, 1)
            else:
                copy_v(s)
                store(s, 1)
                inv = inverse_rms(s, sums)
            rotate(s, inv)

        def transposes(s):
            for t in range(len(x_tiles[s])):
                transpose_x(s, t)

        def prepare(s):
            regroup_x(s)
            quantise_x(s)

        warm_up()
        transposes(0)
        spread_norm_weights()
        transposes(1)
        make_tables(0)
        prepare(0)
        project_step(0)
        prepare(1)
        after_projection(0)
        transposes(2)
        transposes(3)
        make_tables(2)
        project_step(1)
        prepare(2)
        prepare(3)
        after_projection(1)

        for r in range(2, n_steps // 2 + 3):
            first = 2 * r
            for s in (first, first + 1):
                if live(s):
                    transposes(s)
            if live(first):
                make_tables(first)
            if live(first - 2):
                project_step(first - 2)
            early = first - 4 == n_steps - 2
            if early:
                add_halves(first - 4)
                store(first - 4, 0)
            if live(first - 3) and r > 2:
                after_projection(first - 3)
            if live(first - 1):
                project_step(first - 1)
            if live(first):
                prepare(first)
            for s in (first - 4, first - 3):
                if live(s) and not (early and s == first - 4):
                    add_halves(s)
                    store(s, 0)
            if live(first + 1):
                prepare(first + 1)
            if live(first - 2):
                after_projection(first - 2)
